import numpy as np
import ml_dtypes


def mxq(x, axis, fmt="e4m3"):
    dtype, down = {"e4m3": (ml_dtypes.float8_e4m3fn, 7), "e5m2": (ml_dtypes.float8_e5m2, 14)}[fmt]
    v = np.moveaxis(np.asarray(x, np.float32).astype(ml_dtypes.bfloat16).astype(np.float64), axis, -1)
    blocks = v.reshape(v.shape[:-1] + (-1, 32))
    amax = np.abs(blocks).max(-1, keepdims=True)
    byte = np.maximum(np.where(amax > 0, np.frexp(amax)[1] - 1 + 127, 0) - down, 1)
    scale = np.exp2(byte - 127.0)
    codes = (blocks / scale).astype(np.float32).astype(dtype).astype(np.float64)
    return np.moveaxis((codes * scale).reshape(v.shape), -1, axis)


WIDE = False


def mx_kscale(k):
    if not WIDE:
        return np.ones(k)
    levels = np.array([20, -20, 10, -10, 0])
    a = np.random.permutation(np.resize(levels, k // 512 * 4)).reshape(k // 512, 4)
    idx = np.arange(k)
    return np.exp2(a[idx // 512, idx % 128 // 32])


BF16 = ml_dtypes.bfloat16


def bf(x):
    return np.asarray(x, np.float32).astype(BF16)


def f64(x):
    return np.asarray(x).astype(np.float64)


N, M, H, D, R = 1024, 512, 8, 512, 4
GAP = 1e-3
GS = 256.0


def draw(rows, u):
    z = np.random.standard_normal((H, rows, R)) * 1.4 / np.sqrt(R)
    g = np.exp(0.5 * np.random.standard_normal((rows, H, 1)))
    v = (z @ u).transpose(1, 0, 2) + np.random.standard_normal((rows, H, D))
    return bf((v * g).reshape(rows, H * D))


def inv_norms(a, rows):
    v = f64(a).reshape(rows, H, D)
    return 1.0 / np.sqrt((v * v).sum(axis=2))


def cosines(batch_s, batch_ro):
    sn = f64(batch_s).reshape(N, H, D) * inv_norms(batch_s, N)[:, :, None]
    rn = f64(batch_ro).reshape(M, H, D) * inv_norms(batch_ro, M)[:, :, None]
    return sn.transpose(1, 0, 2) @ rn.transpose(1, 2, 0)


def setup_inputs():
    k = mx_kscale(N)[:, None]
    u = np.random.standard_normal((H, R, D))
    s0 = draw(N, u)
    ro = draw(M, u)
    g = np.random.standard_normal((N, M)) * np.exp2(np.random.randint(-12, 1, (N, 1))) * GS
    c = cosines(s0, ro)
    top = np.sort(c, axis=0)
    g = np.where(top[-1] - top[-2] < GAP, 0.0, g)
    return {"batch_s": bf(f64(s0) * k), "batch_ro": ro,
            "dist": np.asarray(c, np.float32),
            "inv_s": np.asarray(inv_norms(s0, N), np.float32),
            "inv_ro": np.asarray(inv_norms(ro, M), np.float32),
            "grad_out": bf(g / k)}


def reference(batch_s, batch_ro, dist, inv_s, inv_ro, grad_out):
    c = f64(dist)
    dd = np.where(c == c.max(axis=0, keepdims=True), f64(grad_out)[None, :, :], 0.0)
    sn = f64(batch_s).reshape(N, H, D) * f64(inv_s)[:, :, None]
    ir = f64(inv_ro)[:, :, None]
    rn = f64(batch_ro).reshape(M, H, D) * ir
    ddq = mxq(dd, 1, "e5m2")
    snq = mxq(sn, 0, "e4m3")
    drn = ddq.transpose(0, 2, 1) @ snq.transpose(1, 0, 2)
    drn = drn.transpose(1, 0, 2)
    t = (rn * drn).sum(axis=2, keepdims=True)
    return ((drn - rn * t) * ir).reshape(M, H * D)

@@ -1,0 +1,175 @@
+import concourse.mybir as mybir
+
+F32 = mybir.dt.float32
+BF16 = mybir.dt.bfloat16
+U32 = mybir.dt.uint32
+U8 = mybir.dt.uint8
+E4M3_X4 = mybir.dt.float8_e4m3fn_x4
+E5M2_X4 = mybir.dt.float8_e5m2_x4
+ALU = mybir.AluOpType
+COPY = mybir.ActivationFunctionType.Copy
+
+P = 128
+PACK = 4
+K_PASS = P * PACK
+N_ROWS = 1024
+M_ROWS = 512
+HEADS = 8
+HEAD_DIM = 512
+PASSES = N_ROWS // K_PASS
+M_TILES = M_ROWS // P
+
+M_PART = 256
+PARTS = M_ROWS // M_PART
+UNIT = PACK * M_PART
+RUN = 4
+HEAD_GROUP = 4
+
+FLOPS = 2 * HEADS * M_ROWS * N_ROWS * HEAD_DIM
+
+
+def by_rows_view(ap):
+    return ap.rearrange("p j (r i) -> p r j i", i=RUN)
+
+
+def grouped_view(ap):
+    return ap.rearrange("p (r i j) -> p r j i", i=RUN, j=PACK)
+
+
+def tile_multiheaddistance_v_kernel(tc, batch_s, batch_ro, dist, inv_s, inv_ro, grad_out, out):
+    nc = tc.nc
+
+    with tc.tile_pool(name="keep", bufs=1) as keep, tc.tile_pool(name="big", bufs=2) as big:
+        dd_codes = keep.tile([P, PASSES, PARTS, HEADS, M_PART], U32, align_bytes=64)
+        dd_scales = keep.tile([P, PASSES, PARTS, HEADS, M_PART], U8, align_bytes=64)
+        sn_codes = keep.tile([P, PASSES, HEADS, HEAD_DIM], U32, align_bytes=64)
+        sn_scales = keep.tile([P, PASSES, HEADS, HEAD_DIM], U8, align_bytes=64)
+        inv_s_sb = keep.tile([P, PASSES, PACK, HEADS], F32)
+        inv_ro_sb = keep.tile([P, M_TILES, HEADS], F32)
+        neg_inv_ro_sq = keep.tile([P, M_TILES, HEADS], F32)
+        neg_coef = keep.tile([P, M_TILES, HEADS], F32)
+        g_grouped = keep.tile([P, PASSES, PACK * M_ROWS], BF16)
+
+        def load_dist_unit(c, part):
+            unit = big.tile([P, HEADS, PACK, M_PART], F32, tag="big")
+            for h in range(HEADS):
+                rows = dist[h, c * K_PASS : (c + 1) * K_PASS, part * M_PART : (part + 1) * M_PART]
+                nc.sync.dma_start(out=unit[:, h], in_=rows.rearrange("(p j) m -> p j m", j=PACK))
+            return unit
+
+        nc.sync.dma_start(
+            out=inv_s_sb[:].rearrange("p c j h -> p c (j h)"),
+            in_=inv_s.rearrange("(c p j) h -> p c (j h)", c=PASSES, j=PACK),
+        )
+        nc.sync.dma_start(out=inv_ro_sb[:], in_=inv_ro.rearrange("(t p) h -> p t h", p=P))
+        nc.vector.scalar_tensor_tensor(
+            out=neg_inv_ro_sq[:], in0=inv_ro_sb[:], scalar=-1.0, in1=inv_ro_sb[:], op0=ALU.mult, op1=ALU.mult
+        )
+
+        units = [(c, part) for c in range(PASSES) for part in range(PARTS)]
+        sn_tiles = [(c, h) for c in range(PASSES) for h in range(HEADS)]
+        SN_PER_UNIT = len(sn_tiles) // len(units)
+
+        with tc.tile_pool(name="rows", bufs=6) as rows_pool, tc.tile_pool(name="work", bufs=2) as work:
+
+            def load_rows(src, c, columns):
+                raw = rows_pool.tile([P, PACK, HEAD_DIM], BF16, tag="raw")
+                nc.sync.dma_start(
+                    out=raw[:], in_=src[c * K_PASS : (c + 1) * K_PASS, columns].rearrange("(p j) w -> p j w", j=PACK)
+                )
+                return raw
+
+            def quantise_sn(c, h, raw):
+                for j in range(PACK):
+                    nc.scalar.activation(
+                        out=raw[:, j], in_=raw[:, j], func=COPY, scale=inv_s_sb[:, c, j, h : h + 1]
+                    )
+                grouped = work.tile([P, PACK * HEAD_DIM], BF16, align_bytes=64, tag="sn_grouped")
+                nc.scalar.copy(out=grouped_view(grouped[:]), in_=by_rows_view(raw[:]))
+                nc.vector.quantize_mx(
+                    out=sn_codes[:, c, h].bitcast(E4M3_X4), scales=sn_scales[:, c, h], in_=grouped[:]
+                )
+
+            def quantise_dd(c, part, unit):
+                top = work.tile([P, HEADS // 2, PACK, M_PART], F32, tag="top", bufs=1)
+                for k in range(HEADS // 2):
+                    nc.vector.tensor_tensor(out=top[:, k], in0=unit[:, 2 * k], in1=unit[:, 2 * k + 1], op=ALU.max)
+                nc.vector.tensor_tensor(out=top[:, 0:2], in0=top[:, 0:2], in1=top[:, 2:4], op=ALU.max)
+                nc.vector.tensor_tensor(out=top[:, 0], in0=top[:, 0], in1=top[:, 1], op=ALU.max)
+                g_unit = g_grouped[:, c, part * UNIT : (part + 1) * UNIT]
+                for first in range(0, HEADS, HEAD_GROUP):
+                    dd = work.tile([P, HEAD_GROUP, UNIT], BF16, align_bytes=64, tag="dd")
+                    for k in range(HEAD_GROUP):
+                        nc.vector.tensor_tensor(
+                            out=grouped_view(dd[:, k]),
+                            in0=by_rows_view(unit[:, first + k]),
+                            in1=by_rows_view(top[:, 0]),
+                            op=ALU.is_equal,
+                        )
+                    nc.vector.tensor_tensor(
+                        out=dd[:], in0=dd[:], in1=g_unit.unsqueeze(1).to_broadcast([P, HEAD_GROUP, UNIT]), op=ALU.mult
+                    )
+                    heads = slice(first, first + HEAD_GROUP)
+                    nc.vector.quantize_mx(
+                        out=dd_codes[:, c, part, heads].rearrange("p h m -> p (h m)").bitcast(E5M2_X4),
+                        scales=dd_scales[:, c, part, heads].rearrange("p h m -> p (h m)"),
+                        in_=dd[:].rearrange("p h e -> p (h e)"),
+                    )
+
+            loaded_units = [load_dist_unit(*units[0])]
+            for c in range(PASSES):
+                g_raw = load_rows(grad_out, c, slice(0, M_ROWS))
+                nc.scalar.copy(out=grouped_view(g_grouped[:, c]), in_=by_rows_view(g_raw[:]))
+            loaded_rows = []
+            for c, h in sn_tiles[:SN_PER_UNIT]:
+                loaded_rows.append(load_rows(batch_s, c, slice(h * HEAD_DIM, (h + 1) * HEAD_DIM)))
+            loaded_units.append(load_dist_unit(*units[1]))
+
+            for u, (c, part) in enumerate(units):
+                quantise_dd(c, part, loaded_units[u])
+                for k in range(u * SN_PER_UNIT, (u + 1) * SN_PER_UNIT):
+                    quantise_sn(sn_tiles[k][0], sn_tiles[k][1], loaded_rows[k])
+                    if k + SN_PER_UNIT < len(sn_tiles):
+                        c_next, h_next = sn_tiles[k + SN_PER_UNIT]
+                        loaded_rows.append(
+                            load_rows(batch_s, c_next, slice(h_next * HEAD_DIM, (h_next + 1) * HEAD_DIM))
+                        )
+                if u + 2 < len(units):
+                    loaded_units.append(load_dist_unit(*units[u + 2]))
+                elif u + 2 == len(units):
+                    ro_sb = big.tile([P, M_TILES, HEADS * HEAD_DIM], BF16, tag="big")
+                    for t in range(M_TILES):
+                        nc.sync.dma_start(out=ro_sb[:, t], in_=batch_ro[t * P : (t + 1) * P, :])
+
+        with tc.tile_pool(name="late", bufs=6) as late, tc.psum_pool(name="psum", bufs=8) as psum:
+            for t in range(M_TILES):
+                part, m_cols = t // 2, slice((t % 2) * P, (t % 2 + 1) * P)
+                for h in range(HEADS):
+                    drn = psum.tile([P, HEAD_DIM], F32)
+                    for c in range(PASSES):
+                        nc.tensor.matmul_mx(
+                            out=drn[:],
+                            lhsT=dd_codes[:, c, part, h, m_cols].bitcast(E5M2_X4),
+                            lhsT_scale=dd_scales[:, c, part, h, m_cols],
+                            rhs=sn_codes[:, c, h].bitcast(E4M3_X4),
+                            rhs_scale=sn_scales[:, c, h],
+                            start=(c == 0),
+                            stop=(c == PASSES - 1),
+                        )
+                    ro = ro_sb[:, t, h * HEAD_DIM : (h + 1) * HEAD_DIM]
+                    y = late.tile([P, HEAD_DIM], F32)
+                    nc.scalar.activation(out=y[:], in_=drn[:], func=COPY, scale=inv_ro_sb[:, t, h : h + 1])
+                    products = late.tile([P, HEAD_DIM], F32, bufs=2)
+                    nc.vector.scalar_tensor_tensor(
+                        out=products[:],
+                        in0=y[:],
+                        scalar=neg_inv_ro_sq[:, t, h : h + 1],
+                        in1=ro,
+                        op0=ALU.mult,
+                        op1=ALU.mult,
+                        accum_out=neg_coef[:, t, h : h + 1],
+                    )
+                    nc.vector.scalar_tensor_tensor(
+                        out=y[:], in0=ro, scalar=neg_coef[:, t, h : h + 1], in1=y[:], op0=ALU.mult, op1=ALU.add
+                    )
+                    nc.sync.dma_start(out=out[t * P : (t + 1) * P, h * HEAD_DIM : (h + 1) * HEAD_DIM], in_=y[:])

@@ -24,6 +24,7 @@ PARTS = M_ROWS // M_PART
 UNIT = PACK * M_PART
 RUN = 4
 HEAD_GROUP = 4
+GPSIMD_EVERY = 4
 
 FLOPS = 2 * HEADS * M_ROWS * N_ROWS * HEAD_DIM
 
@@ -47,7 +48,8 @@ def tile_multiheaddistance_v_kernel(tc, batch_s, batch_ro, dist, inv_s, inv_ro, 
         inv_s_sb = keep.tile([P, PASSES, PACK, HEADS], F32)
         inv_ro_sb = keep.tile([P, M_TILES, HEADS], F32)
         neg_inv_ro_sq = keep.tile([P, M_TILES, HEADS], F32)
-        neg_coef = keep.tile([P, M_TILES, HEADS], F32)
+        coef_v = keep.tile([P, M_TILES, HEADS], F32)
+        coef_g = keep.tile([P, M_TILES, HEADS], F32)
         g_grouped = keep.tile([P, PASSES, PACK * M_ROWS], BF16)
 
         def load_dist_unit(c, part):
@@ -91,25 +93,31 @@ def tile_multiheaddistance_v_kernel(tc, batch_s, batch_ro, dist, inv_s, inv_ro, 
                 )
 
             def quantise_dd(c, part, unit):
-                top = work.tile([P, HEADS // 2, PACK, M_PART], F32, tag="top", bufs=1)
-                for k in range(HEADS // 2):
-                    nc.vector.tensor_tensor(out=top[:, k], in0=unit[:, 2 * k], in1=unit[:, 2 * k + 1], op=ALU.max)
-                nc.vector.tensor_tensor(out=top[:, 0:2], in0=top[:, 0:2], in1=top[:, 2:4], op=ALU.max)
-                nc.vector.tensor_tensor(out=top[:, 0], in0=top[:, 0], in1=top[:, 1], op=ALU.max)
+                best = work.tile([P, 2, PACK, M_PART], F32, tag="best")
+                for k in range(2):
+                    nc.vector.tensor_tensor(out=best[:, k], in0=unit[:, 2 * k], in1=unit[:, 2 * k + 1], op=ALU.max)
+                for h in range(4, HEADS):
+                    nc.vector.tensor_tensor(out=best[:, h % 2], in0=best[:, h % 2], in1=unit[:, h], op=ALU.max)
+                top = best[:, 0]
+                nc.vector.tensor_tensor(out=top, in0=best[:, 0], in1=best[:, 1], op=ALU.max)
                 g_unit = g_grouped[:, c, part * UNIT : (part + 1) * UNIT]
+                dd_groups = []
                 for first in range(0, HEADS, HEAD_GROUP):
-                    dd = work.tile([P, HEAD_GROUP, UNIT], BF16, align_bytes=64, tag="dd")
+                    dd = work.tile([P, HEAD_GROUP, UNIT], BF16, align_bytes=64, tag="dd", bufs=3)
+                    dd_groups.append(dd)
                     for k in range(HEAD_GROUP):
                         nc.vector.tensor_tensor(
                             out=grouped_view(dd[:, k]),
                             in0=by_rows_view(unit[:, first + k]),
-                            in1=by_rows_view(top[:, 0]),
+                            in1=by_rows_view(top),
                             op=ALU.is_equal,
                         )
+                for dd in dd_groups:
                     nc.vector.tensor_tensor(
                         out=dd[:], in0=dd[:], in1=g_unit.unsqueeze(1).to_broadcast([P, HEAD_GROUP, UNIT]), op=ALU.mult
                     )
-                    heads = slice(first, first + HEAD_GROUP)
+                for k, dd in enumerate(dd_groups):
+                    heads = slice(k * HEAD_GROUP, (k + 1) * HEAD_GROUP)
                     nc.vector.quantize_mx(
                         out=dd_codes[:, c, part, heads].rearrange("p h m -> p (h m)").bitcast(E5M2_X4),
                         scales=dd_scales[:, c, part, heads].rearrange("p h m -> p (h m)"),
@@ -141,35 +149,82 @@ def tile_multiheaddistance_v_kernel(tc, batch_s, batch_ro, dist, inv_s, inv_ro, 
                     for t in range(M_TILES):
                         nc.sync.dma_start(out=ro_sb[:, t], in_=batch_ro[t * P : (t + 1) * P, :])
 
-        with tc.tile_pool(name="late", bufs=6) as late, tc.psum_pool(name="psum", bufs=8) as psum:
-            for t in range(M_TILES):
+        tiles = [(t, h) for t in range(M_TILES) for h in range(HEADS)]
+        groups = [tiles[k : k + GPSIMD_EVERY] for k in range(0, len(tiles), GPSIMD_EVERY)]
+
+        with tc.tile_pool(name="late", bufs=3) as late, tc.psum_pool(name="psum", bufs=8) as psum:
+
+            def ro_of(t, h):
+                return ro_sb[:, t, h * HEAD_DIM : (h + 1) * HEAD_DIM]
+
+            def store(t, h, result):
+                nc.sync.dma_start(out=out[t * P : (t + 1) * P, h * HEAD_DIM : (h + 1) * HEAD_DIM], in_=result[:])
+
+            def multiply(t, h):
                 part, m_cols = t // 2, slice((t % 2) * P, (t % 2 + 1) * P)
-                for h in range(HEADS):
-                    drn = psum.tile([P, HEAD_DIM], F32)
-                    for c in range(PASSES):
-                        nc.tensor.matmul_mx(
-                            out=drn[:],
-                            lhsT=dd_codes[:, c, part, h, m_cols].bitcast(E5M2_X4),
-                            lhsT_scale=dd_scales[:, c, part, h, m_cols],
-                            rhs=sn_codes[:, c, h].bitcast(E4M3_X4),
-                            rhs_scale=sn_scales[:, c, h],
-                            start=(c == 0),
-                            stop=(c == PASSES - 1),
-                        )
-                    ro = ro_sb[:, t, h * HEAD_DIM : (h + 1) * HEAD_DIM]
-                    y = late.tile([P, HEAD_DIM], F32)
-                    nc.scalar.activation(out=y[:], in_=drn[:], func=COPY, scale=inv_ro_sb[:, t, h : h + 1])
-                    products = late.tile([P, HEAD_DIM], F32, bufs=2)
+                drn = psum.tile([P, HEAD_DIM], F32, tag="drn")
+                for c in range(PASSES):
+                    nc.tensor.matmul_mx(
+                        out=drn[:],
+                        lhsT=dd_codes[:, c, part, h, m_cols].bitcast(E5M2_X4),
+                        lhsT_scale=dd_scales[:, c, part, h, m_cols],
+                        rhs=sn_codes[:, c, h].bitcast(E4M3_X4),
+                        rhs_scale=sn_scales[:, c, h],
+                        start=(c == 0),
+                        stop=(c == PASSES - 1),
+                    )
+                return drn
+
+            def first_half(group):
+                drns = [multiply(t, h) for t, h in group]
+                t, h = group[0]
+                y = late.tile([P, HEAD_DIM], F32, tag="y")
+                nc.scalar.activation(out=y[:], in_=drns[0][:], func=COPY, scale=inv_ro_sb[:, t, h : h + 1])
+                products = late.tile([P, HEAD_DIM], F32, tag="products_g")
+                nc.gpsimd.tensor_tensor(out=products[:], in0=y[:], in1=ro_of(t, h), op=ALU.mult)
+                for (t, h), drn in zip(group[1:], drns[1:]):
+                    unused = late.tile([P, HEAD_DIM], F32, tag="products_v")
                     nc.vector.scalar_tensor_tensor(
-                        out=products[:],
-                        in0=y[:],
+                        out=unused[:],
+                        in0=drn[:],
                         scalar=neg_inv_ro_sq[:, t, h : h + 1],
-                        in1=ro,
+                        in1=ro_of(t, h),
                         op0=ALU.mult,
                         op1=ALU.mult,
-                        accum_out=neg_coef[:, t, h : h + 1],
+                        accum_out=coef_v[:, t, h : h + 1],
                     )
+                results = []
+                for (t, h), drn in zip(group[1:], drns[1:]):
+                    result = late.tile([P, HEAD_DIM], F32, tag="result_v", bufs=3 * GPSIMD_EVERY)
                     nc.vector.scalar_tensor_tensor(
-                        out=y[:], in0=ro, scalar=neg_coef[:, t, h : h + 1], in1=y[:], op0=ALU.mult, op1=ALU.add
+                        out=result[:], in0=ro_of(t, h), scalar=coef_v[:, t, h : h + 1], in1=drn[:], op0=ALU.mult, op1=ALU.add
                     )
-                    nc.sync.dma_start(out=out[t * P : (t + 1) * P, h * HEAD_DIM : (h + 1) * HEAD_DIM], in_=y[:])
+                    results.append(result)
+                return y, products, results
+
+            def second_half(group, y, products, results):
+                t, h = group[0]
+                nc.scalar.activation(
+                    out=products[:],
+                    in_=products[:],
+                    func=COPY,
+                    scale=neg_inv_ro_sq[:, t, h : h + 1],
+                    accum_out=coef_g[:, t, h : h + 1],
+                )
+                result = late.tile([P, HEAD_DIM], F32, tag="result_g")
+                nc.gpsimd.tensor_scalar(
+                    out=result[:], in0=ro_of(t, h), scalar1=coef_g[:, t, h : h + 1], scalar2=0.0, op0=ALU.mult, op1=ALU.add
+                )
+                nc.gpsimd.tensor_tensor(out=result[:], in0=result[:], in1=y[:], op=ALU.add)
+                for (t, h), result_v in zip(group[1:], results):
+                    nc.scalar.activation(out=result_v[:], in_=result_v[:], func=COPY, scale=inv_ro_sb[:, t, h : h + 1])
+                    store(t, h, result_v)
+                store(group[0][0], group[0][1], result)
+
+            with tc.manual_schedule():
+                halfway = first_half(groups[0])
+                for k in range(1, len(groups)):
+                    ahead = first_half(groups[k])
+                    second_half(groups[k - 1], *halfway)
+                    halfway = ahead
+                second_half(groups[-1], *halfway)

@@ -59,20 +59,13 @@ def tile_multiheaddistance_v_kernel(tc, batch_s, batch_ro, dist, inv_s, inv_ro, 
                 nc.sync.dma_start(out=unit[:, h], in_=rows.rearrange("(p j) m -> p j m", j=PACK))
             return unit
 
-        nc.sync.dma_start(
-            out=inv_s_sb[:].rearrange("p c j h -> p c (j h)"),
-            in_=inv_s.rearrange("(c p j) h -> p c (j h)", c=PASSES, j=PACK),
-        )
-        nc.sync.dma_start(out=inv_ro_sb[:], in_=inv_ro.rearrange("(t p) h -> p t h", p=P))
-        nc.vector.scalar_tensor_tensor(
-            out=neg_inv_ro_sq[:], in0=inv_ro_sb[:], scalar=-1.0, in1=inv_ro_sb[:], op0=ALU.mult, op1=ALU.mult
-        )
-
         units = [(c, part) for c in range(PASSES) for part in range(PARTS)]
         sn_tiles = [(c, h) for c in range(PASSES) for h in range(HEADS)]
         SN_PER_UNIT = len(sn_tiles) // len(units)
 
-        with tc.tile_pool(name="rows", bufs=6) as rows_pool, tc.tile_pool(name="work", bufs=2) as work:
+        with tc.tile_pool(name="rows", bufs=6) as rows_pool, tc.tile_pool(
+            name="work", bufs=1
+        ) as work, tc.manual_schedule():
 
             def load_rows(src, c, columns):
                 raw = rows_pool.tile([P, PACK, HEAD_DIM], BF16, tag="raw")
@@ -81,29 +74,42 @@ def tile_multiheaddistance_v_kernel(tc, batch_s, batch_ro, dist, inv_s, inv_ro, 
                 )
                 return raw
 
-            def quantise_sn(c, h, raw):
+            def load_sn_rows(k):
+                c, h = sn_tiles[k]
+                return load_rows(batch_s, c, slice(h * HEAD_DIM, (h + 1) * HEAD_DIM))
+
+            def scale_and_regroup_sn(k, raw):
+                c, h = sn_tiles[k]
                 for j in range(PACK):
                     nc.scalar.activation(
                         out=raw[:, j], in_=raw[:, j], func=COPY, scale=inv_s_sb[:, c, j, h : h + 1]
                     )
-                grouped = work.tile([P, PACK * HEAD_DIM], BF16, align_bytes=64, tag="sn_grouped")
+                grouped = work.tile([P, PACK * HEAD_DIM], BF16, align_bytes=64, tag="sn_grouped", bufs=6)
                 nc.scalar.copy(out=grouped_view(grouped[:]), in_=by_rows_view(raw[:]))
+                return grouped
+
+            def quantise_sn(k, grouped):
+                c, h = sn_tiles[k]
                 nc.vector.quantize_mx(
                     out=sn_codes[:, c, h].bitcast(E4M3_X4), scales=sn_scales[:, c, h], in_=grouped[:]
                 )
 
-            def quantise_dd(c, part, unit):
+            def quantise_dd(c, part, unit, waiting):
                 best = work.tile([P, 2, PACK, M_PART], F32, tag="best")
                 for k in range(2):
                     nc.vector.tensor_tensor(out=best[:, k], in0=unit[:, 2 * k], in1=unit[:, 2 * k + 1], op=ALU.max)
                 for h in range(4, HEADS):
                     nc.vector.tensor_tensor(out=best[:, h % 2], in0=best[:, h % 2], in1=unit[:, h], op=ALU.max)
+                for k, grouped in waiting[0:1]:
+                    quantise_sn(k, grouped)
                 top = best[:, 0]
                 nc.vector.tensor_tensor(out=top, in0=best[:, 0], in1=best[:, 1], op=ALU.max)
+                for k, grouped in waiting[1:2]:
+                    quantise_sn(k, grouped)
                 g_unit = g_grouped[:, c, part * UNIT : (part + 1) * UNIT]
                 dd_groups = []
                 for first in range(0, HEADS, HEAD_GROUP):
-                    dd = work.tile([P, HEAD_GROUP, UNIT], BF16, align_bytes=64, tag="dd", bufs=3)
+                    dd = work.tile([P, HEAD_GROUP, UNIT], BF16, align_bytes=64, tag="dd", bufs=2)
                     dd_groups.append(dd)
                     for k in range(HEAD_GROUP):
                         nc.vector.tensor_tensor(
@@ -123,31 +129,41 @@ def tile_multiheaddistance_v_kernel(tc, batch_s, batch_ro, dist, inv_s, inv_ro, 
                         scales=dd_scales[:, c, part, heads].rearrange("p h m -> p (h m)"),
                         in_=dd[:].rearrange("p h e -> p (h e)"),
                     )
+                for k, grouped in waiting[2:]:
+                    quantise_sn(k, grouped)
 
             loaded_units = [load_dist_unit(*units[0])]
+            nc.sync.dma_start(
+                out=inv_s_sb[:].rearrange("p c j h -> p c (j h)"),
+                in_=inv_s.rearrange("(c p j) h -> p c (j h)", c=PASSES, j=PACK),
+            )
             for c in range(PASSES):
                 g_raw = load_rows(grad_out, c, slice(0, M_ROWS))
                 nc.scalar.copy(out=grouped_view(g_grouped[:, c]), in_=by_rows_view(g_raw[:]))
-            loaded_rows = []
-            for c, h in sn_tiles[:SN_PER_UNIT]:
-                loaded_rows.append(load_rows(batch_s, c, slice(h * HEAD_DIM, (h + 1) * HEAD_DIM)))
+            loaded_rows = [load_sn_rows(k) for k in range(SN_PER_UNIT // 2)]
             loaded_units.append(load_dist_unit(*units[1]))
+            loaded_rows.extend([load_sn_rows(k) for k in range(SN_PER_UNIT // 2, SN_PER_UNIT)])
+            nc.sync.dma_start(out=inv_ro_sb[:], in_=inv_ro.rearrange("(t p) h -> p t h", p=P))
 
+            waiting = []
             for u, (c, part) in enumerate(units):
-                quantise_dd(c, part, loaded_units[u])
+                quantise_dd(c, part, loaded_units[u], waiting)
+                waiting = []
                 for k in range(u * SN_PER_UNIT, (u + 1) * SN_PER_UNIT):
-                    quantise_sn(sn_tiles[k][0], sn_tiles[k][1], loaded_rows[k])
+                    waiting.append((k, scale_and_regroup_sn(k, loaded_rows[k])))
                     if k + SN_PER_UNIT < len(sn_tiles):
-                        c_next, h_next = sn_tiles[k + SN_PER_UNIT]
-                        loaded_rows.append(
-                            load_rows(batch_s, c_next, slice(h_next * HEAD_DIM, (h_next + 1) * HEAD_DIM))
-                        )
+                        loaded_rows.append(load_sn_rows(k + SN_PER_UNIT))
                 if u + 2 < len(units):
                     loaded_units.append(load_dist_unit(*units[u + 2]))
                 elif u + 2 == len(units):
                     ro_sb = big.tile([P, M_TILES, HEADS * HEAD_DIM], BF16, tag="big")
                     for t in range(M_TILES):
                         nc.sync.dma_start(out=ro_sb[:, t], in_=batch_ro[t * P : (t + 1) * P, :])
+            for k, grouped in waiting:
+                quantise_sn(k, grouped)
+            nc.vector.scalar_tensor_tensor(
+                out=neg_inv_ro_sq[:], in0=inv_ro_sb[:], scalar=-1.0, in1=inv_ro_sb[:], op0=ALU.mult, op1=ALU.mult
+            )
 
         tiles = [(t, h) for t in range(M_TILES) for h in range(HEADS)]
         groups = [tiles[k : k + GPSIMD_EVERY] for k in range(0, len(tiles), GPSIMD_EVERY)]

@@ -1,4 +1,5 @@
 import concourse.mybir as mybir
+from concourse.masks import make_identity
 
 F32 = mybir.dt.float32
 BF16 = mybir.dt.bfloat16
@@ -24,6 +25,9 @@ PARTS = M_ROWS // M_PART
 UNIT = PACK * M_PART
 RUN = 4
 HEAD_GROUP = 4
+HALVES = M_PART // P
+HALF = PACK * P
+GPSIMD_HEADS = 3
 GPSIMD_EVERY = 4
 
 FLOPS = 2 * HEADS * M_ROWS * N_ROWS * HEAD_DIM
@@ -63,9 +67,12 @@ def tile_multiheaddistance_v_kernel(tc, batch_s, batch_ro, dist, inv_s, inv_ro, 
         sn_tiles = [(c, h) for c in range(PASSES) for h in range(HEADS)]
         SN_PER_UNIT = len(sn_tiles) // len(units)
 
+        identity = keep.tile([P, P], F32)
+        make_identity(nc, identity[:])
+
         with tc.tile_pool(name="rows", bufs=6) as rows_pool, tc.tile_pool(
             name="work", bufs=1
-        ) as work, tc.manual_schedule():
+        ) as work, tc.psum_pool(name="top_psum", bufs=2 * HALVES) as top_psum, tc.manual_schedule():
 
             def load_rows(src, c, columns):
                 raw = rows_pool.tile([P, PACK, HEAD_DIM], BF16, tag="raw")
@@ -88,39 +95,58 @@ def tile_multiheaddistance_v_kernel(tc, batch_s, batch_ro, dist, inv_s, inv_ro, 
                 nc.scalar.copy(out=grouped_view(grouped[:]), in_=by_rows_view(raw[:]))
                 return grouped
 
-            def quantise_sn(k, grouped):
-                c, h = sn_tiles[k]
-                nc.vector.quantize_mx(
-                    out=sn_codes[:, c, h].bitcast(E4M3_X4), scales=sn_scales[:, c, h], in_=grouped[:]
-                )
+            def quantise_sn(tiles):
+                for k, grouped in tiles:
+                    c, h = sn_tiles[k]
+                    nc.vector.quantize_mx(
+                        out=sn_codes[:, c, h].bitcast(E4M3_X4), scales=sn_scales[:, c, h], in_=grouped[:]
+                    )
 
-            def quantise_dd(c, part, unit, waiting):
+            def maximum(unit, fillers):
                 best = work.tile([P, 2, PACK, M_PART], F32, tag="best")
                 for k in range(2):
                     nc.vector.tensor_tensor(out=best[:, k], in0=unit[:, 2 * k], in1=unit[:, 2 * k + 1], op=ALU.max)
                 for h in range(4, HEADS):
                     nc.vector.tensor_tensor(out=best[:, h % 2], in0=best[:, h % 2], in1=unit[:, h], op=ALU.max)
-                for k, grouped in waiting[0:1]:
-                    quantise_sn(k, grouped)
-                top = best[:, 0]
-                nc.vector.tensor_tensor(out=top, in0=best[:, 0], in1=best[:, 1], op=ALU.max)
-                for k, grouped in waiting[1:2]:
-                    quantise_sn(k, grouped)
+                quantise_sn(fillers)
+                nc.vector.tensor_tensor(out=best[:, 0], in0=best[:, 0], in1=best[:, 1], op=ALU.max)
+                return [best[:, 0, :, b * P : (b + 1) * P] for b in range(HALVES)]
+
+            def to_psum(top_halves):
+                banks = []
+                for half in top_halves:
+                    bank = top_psum.tile([P, PACK, P], F32, tag="top")
+                    nc.tensor.matmul(out=bank[:], lhsT=identity[:], rhs=half, start=True, stop=True)
+                    banks.append(bank[:])
+                return banks
+
+            def compare(c, part, unit, top_halves, gpsimd_heads):
                 g_unit = g_grouped[:, c, part * UNIT : (part + 1) * UNIT]
                 dd_groups = []
                 for first in range(0, HEADS, HEAD_GROUP):
                     dd = work.tile([P, HEAD_GROUP, UNIT], BF16, align_bytes=64, tag="dd", bufs=2)
                     dd_groups.append(dd)
                     for k in range(HEAD_GROUP):
-                        nc.vector.tensor_tensor(
-                            out=grouped_view(dd[:, k]),
-                            in0=by_rows_view(unit[:, first + k]),
-                            in1=by_rows_view(top),
-                            op=ALU.is_equal,
-                        )
-                for dd in dd_groups:
+                        for b in range(HALVES):
+                            nc.vector.tensor_tensor(
+                                out=grouped_view(dd[:, k, b * HALF : (b + 1) * HALF]),
+                                in0=by_rows_view(unit[:, first + k, :, b * P : (b + 1) * P]),
+                                in1=by_rows_view(top_halves[b]),
+                                op=ALU.is_equal,
+                            )
+                        if first + k < gpsimd_heads:
+                            nc.gpsimd.tensor_tensor(out=dd[:, k], in0=dd[:, k], in1=g_unit, op=ALU.mult)
+                return dd_groups
+
+            def multiply_and_quantise(c, part, dd_groups, gpsimd_heads, fillers):
+                g_unit = g_grouped[:, c, part * UNIT : (part + 1) * UNIT]
+                for k, dd in enumerate(dd_groups):
+                    done = max(0, gpsimd_heads - k * HEAD_GROUP)
                     nc.vector.tensor_tensor(
-                        out=dd[:], in0=dd[:], in1=g_unit.unsqueeze(1).to_broadcast([P, HEAD_GROUP, UNIT]), op=ALU.mult
+                        out=dd[:, done:],
+                        in0=dd[:, done:],
+                        in1=g_unit.unsqueeze(1).to_broadcast([P, HEAD_GROUP - done, UNIT]),
+                        op=ALU.mult,
                     )
                 for k, dd in enumerate(dd_groups):
                     heads = slice(k * HEAD_GROUP, (k + 1) * HEAD_GROUP)
@@ -129,8 +155,7 @@ def tile_multiheaddistance_v_kernel(tc, batch_s, batch_ro, dist, inv_s, inv_ro, 
                         scales=dd_scales[:, c, part, heads].rearrange("p h m -> p (h m)"),
                         in_=dd[:].rearrange("p h e -> p (h e)"),
                     )
-                for k, grouped in waiting[2:]:
-                    quantise_sn(k, grouped)
+                quantise_sn(fillers)
 
             loaded_units = [load_dist_unit(*units[0])]
             nc.sync.dma_start(
@@ -145,9 +170,15 @@ def tile_multiheaddistance_v_kernel(tc, batch_s, batch_ro, dist, inv_s, inv_ro, 
             loaded_rows.extend([load_sn_rows(k) for k in range(SN_PER_UNIT // 2, SN_PER_UNIT)])
             nc.sync.dma_start(out=inv_ro_sb[:], in_=inv_ro.rearrange("(t p) h -> p t h", p=P))
 
+            shares = [0] + [GPSIMD_HEADS] * (len(units) - 1)
+            dd_groups = compare(*units[0], loaded_units[0], maximum(loaded_units[0], []), shares[0])
             waiting = []
             for u, (c, part) in enumerate(units):
-                quantise_dd(c, part, loaded_units[u], waiting)
+                if u + 1 < len(units):
+                    top_banks = to_psum(maximum(loaded_units[u + 1], waiting[0:2]))
+                else:
+                    quantise_sn(waiting[0:2])
+                multiply_and_quantise(c, part, dd_groups, shares[u], waiting[2:])
                 waiting = []
                 for k in range(u * SN_PER_UNIT, (u + 1) * SN_PER_UNIT):
                     waiting.append((k, scale_and_regroup_sn(k, loaded_rows[k])))
@@ -159,8 +190,9 @@ def tile_multiheaddistance_v_kernel(tc, batch_s, batch_ro, dist, inv_s, inv_ro, 
                     ro_sb = big.tile([P, M_TILES, HEADS * HEAD_DIM], BF16, tag="big")
                     for t in range(M_TILES):
                         nc.sync.dma_start(out=ro_sb[:, t], in_=batch_ro[t * P : (t + 1) * P, :])
-            for k, grouped in waiting:
-                quantise_sn(k, grouped)
+                if u + 1 < len(units):
+                    dd_groups = compare(*units[u + 1], loaded_units[u + 1], top_banks, shares[u + 1])
+            quantise_sn(waiting)
             nc.vector.scalar_tensor_tensor(
                 out=neg_inv_ro_sq[:], in0=inv_ro_sb[:], scalar=-1.0, in1=inv_ro_sb[:], op0=ALU.mult, op1=ALU.mult
             )

@@ -9,6 +9,7 @@ E4M3_X4 = mybir.dt.float8_e4m3fn_x4
 E5M2_X4 = mybir.dt.float8_e5m2_x4
 ALU = mybir.AluOpType
 COPY = mybir.ActivationFunctionType.Copy
+RELU = mybir.ActivationFunctionType.Relu
 
 P = 128
 PACK = 4
@@ -23,12 +24,14 @@ M_TILES = M_ROWS // P
 M_PART = 256
 PARTS = M_ROWS // M_PART
 UNIT = PACK * M_PART
+HALVES = M_PART // P
 RUN = 4
 HEAD_GROUP = 4
-HALVES = M_PART // P
-HALF = PACK * P
-GPSIMD_HEADS = 3
 GPSIMD_EVERY = 4
+BIG = 2.0 ** 100
+STREAM_BUFS = 16
+RO_HEADS = 4
+LAG = 2
 
 FLOPS = 2 * HEADS * M_ROWS * N_ROWS * HEAD_DIM
 
@@ -44,7 +47,7 @@ def grouped_view(ap):
 def tile_multiheaddistance_v_kernel(tc, batch_s, batch_ro, dist, inv_s, inv_ro, grad_out, out):
     nc = tc.nc
 
-    with tc.tile_pool(name="keep", bufs=1) as keep, tc.tile_pool(name="big", bufs=2) as big:
+    with tc.tile_pool(name="keep", bufs=1) as keep, tc.tile_pool(name="stream", bufs=STREAM_BUFS) as stream:
         dd_codes = keep.tile([P, PASSES, PARTS, HEADS, M_PART], U32, align_bytes=64)
         dd_scales = keep.tile([P, PASSES, PARTS, HEADS, M_PART], U8, align_bytes=64)
         sn_codes = keep.tile([P, PASSES, HEADS, HEAD_DIM], U32, align_bytes=64)
@@ -55,24 +58,34 @@ def tile_multiheaddistance_v_kernel(tc, batch_s, batch_ro, dist, inv_s, inv_ro, 
         coef_v = keep.tile([P, M_TILES, HEADS], F32)
         coef_g = keep.tile([P, M_TILES, HEADS], F32)
         g_grouped = keep.tile([P, PASSES, PACK * M_ROWS], BF16)
-
-        def load_dist_unit(c, part):
-            unit = big.tile([P, HEADS, PACK, M_PART], F32, tag="big")
-            for h in range(HEADS):
-                rows = dist[h, c * K_PASS : (c + 1) * K_PASS, part * M_PART : (part + 1) * M_PART]
-                nc.sync.dma_start(out=unit[:, h], in_=rows.rearrange("(p j) m -> p j m", j=PACK))
-            return unit
-
-        units = [(c, part) for c in range(PASSES) for part in range(PARTS)]
-        sn_tiles = [(c, h) for c in range(PASSES) for h in range(HEADS)]
-        SN_PER_UNIT = len(sn_tiles) // len(units)
-
         identity = keep.tile([P, P], F32)
         make_identity(nc, identity[:])
 
+        units = [(c, part) for c in range(PASSES) for part in range(PARTS)]
+        sn_tiles = [(c, h) for c in range(PASSES) for h in range(HEADS)]
+        SLOTS = len(units) * HEADS
+
+        heads = {}
+        best = {}
+        minus_top = {}
+        diffs = {}
+        turned = {}
+        words = {}
+        dd_tiles = {}
+        raws = {}
+        groupeds = {}
+        ro_tiles = []
+
         with tc.tile_pool(name="rows", bufs=6) as rows_pool, tc.tile_pool(
             name="work", bufs=1
-        ) as work, tc.psum_pool(name="top_psum", bufs=2 * HALVES) as top_psum, tc.manual_schedule():
+        ) as work, tc.psum_pool(name="turn", bufs=4) as turn, tc.manual_schedule():
+
+            def load_head(u, h):
+                c, part = units[u]
+                tile = stream.tile([P, PACK, M_PART], F32, tag="stream")
+                rows = dist[h, c * K_PASS : (c + 1) * K_PASS, part * M_PART : (part + 1) * M_PART]
+                nc.sync.dma_start(out=tile[:], in_=rows.rearrange("(p j) m -> p j m", j=PACK))
+                heads[(u, h)] = tile
 
             def load_rows(src, c, columns):
                 raw = rows_pool.tile([P, PACK, HEAD_DIM], BF16, tag="raw")
@@ -83,116 +96,160 @@ def tile_multiheaddistance_v_kernel(tc, batch_s, batch_ro, dist, inv_s, inv_ro, 
 
             def load_sn_rows(k):
                 c, h = sn_tiles[k]
-                return load_rows(batch_s, c, slice(h * HEAD_DIM, (h + 1) * HEAD_DIM))
+                raws[k] = load_rows(batch_s, c, slice(h * HEAD_DIM, (h + 1) * HEAD_DIM))
 
-            def scale_and_regroup_sn(k, raw):
-                c, h = sn_tiles[k]
+            def load_ro(k):
+                t, half = k // (HEADS // RO_HEADS), k % (HEADS // RO_HEADS)
+                tile = stream.tile([P, RO_HEADS * HEAD_DIM], BF16, tag="stream")
+                width = RO_HEADS * HEAD_DIM
+                nc.sync.dma_start(out=tile[:], in_=batch_ro[t * P : (t + 1) * P, half * width : (half + 1) * width])
+                ro_tiles.append(tile)
+
+            def regroup_g(c, g_raw):
+                nc.scalar.copy(out=grouped_view(g_grouped[:, c]), in_=by_rows_view(g_raw[:]))
+
+            def maximum_step(u, i):
+                if i == 0:
+                    tile = work.tile([P, 2, PACK, M_PART], F32, tag="best")
+                    best[u] = tile
+                b = best[u]
+                if i < 2:
+                    nc.vector.tensor_tensor(out=b[:, i], in0=heads[(u, 2 * i)][:], in1=heads[(u, 2 * i + 1)][:], op=ALU.max)
+                elif i < 6:
+                    nc.vector.tensor_tensor(out=b[:, i % 2], in0=b[:, i % 2], in1=heads[(u, i + 2)][:], op=ALU.max)
+                elif i == 6:
+                    nc.vector.tensor_tensor(out=b[:, 0], in0=b[:, 0], in1=b[:, 1], op=ALU.max)
+                else:
+                    tile = work.tile([P, PACK, M_PART], F32, tag="minus_top", bufs=2)
+                    nc.vector.tensor_scalar_mul(out=tile[:], in0=b[:, 0], scalar1=-1.0)
+                    minus_top[u] = tile
+
+            def turn_and_subtract(u, h, b):
+                cols = slice(b * P, (b + 1) * P)
+                diff = turn.tile([P, PACK, P], F32, tag="diff")
                 for j in range(PACK):
-                    nc.scalar.activation(
-                        out=raw[:, j], in_=raw[:, j], func=COPY, scale=inv_s_sb[:, c, j, h : h + 1]
+                    nc.tensor.matmul(
+                        out=diff[:, j], lhsT=heads[(u, h)][:, j, cols], rhs=identity[:], is_transpose=True, start=True, stop=False
                     )
-                grouped = work.tile([P, PACK * HEAD_DIM], BF16, align_bytes=64, tag="sn_grouped", bufs=6)
-                nc.scalar.copy(out=grouped_view(grouped[:]), in_=by_rows_view(raw[:]))
-                return grouped
-
-            def quantise_sn(tiles):
-                for k, grouped in tiles:
-                    c, h = sn_tiles[k]
-                    nc.vector.quantize_mx(
-                        out=sn_codes[:, c, h].bitcast(E4M3_X4), scales=sn_scales[:, c, h], in_=grouped[:]
+                    nc.tensor.matmul(
+                        out=diff[:, j], lhsT=minus_top[u][:, j, cols], rhs=identity[:], is_transpose=True, start=False, stop=True
                     )
+                diffs[(u, h, b)] = diff
 
-            def maximum(unit, fillers):
-                best = work.tile([P, 2, PACK, M_PART], F32, tag="best")
-                for k in range(2):
-                    nc.vector.tensor_tensor(out=best[:, k], in0=unit[:, 2 * k], in1=unit[:, 2 * k + 1], op=ALU.max)
-                for h in range(4, HEADS):
-                    nc.vector.tensor_tensor(out=best[:, h % 2], in0=best[:, h % 2], in1=unit[:, h], op=ALU.max)
-                quantise_sn(fillers)
-                nc.vector.tensor_tensor(out=best[:, 0], in0=best[:, 0], in1=best[:, 1], op=ALU.max)
-                return [best[:, 0, :, b * P : (b + 1) * P] for b in range(HALVES)]
+            def mask(u, h, b):
+                tile = work.tile([P, 2, P, 2], BF16, tag="turned", bufs=4)
+                nc.scalar.activation(
+                    out=tile[:], in_=diffs[(u, h, b)][:].rearrange("m (u e) p -> m u p e", e=2), func=RELU, scale=BIG, bias=1.0
+                )
+                turned[(u, h, b)] = tile
 
-            def to_psum(top_halves):
-                banks = []
-                for half in top_halves:
-                    bank = top_psum.tile([P, PACK, P], F32, tag="top")
-                    nc.tensor.matmul(out=bank[:], lhsT=identity[:], rhs=half, start=True, stop=True)
-                    banks.append(bank[:])
-                return banks
+            def turn_back(u, h, b):
+                if b == 0:
+                    tile = turn.tile([P, HALVES, P, 2], F32, tag="mask")
+                    words[(u, h)] = tile
+                pairs = turned[(u, h, b)][:].rearrange("m u p e -> m (u p e)").bitcast(F32)
+                for u2 in range(2):
+                    nc.tensor.transpose(out=words[(u, h)][:, b, :, u2], in_=pairs[:, u2 * P : (u2 + 1) * P], identity=identity[:])
 
-            def compare(c, part, unit, top_halves, gpsimd_heads):
-                g_unit = g_grouped[:, c, part * UNIT : (part + 1) * UNIT]
-                dd_groups = []
-                for first in range(0, HEADS, HEAD_GROUP):
-                    dd = work.tile([P, HEAD_GROUP, UNIT], BF16, align_bytes=64, tag="dd", bufs=2)
-                    dd_groups.append(dd)
-                    for k in range(HEAD_GROUP):
-                        for b in range(HALVES):
-                            nc.vector.tensor_tensor(
-                                out=grouped_view(dd[:, k, b * HALF : (b + 1) * HALF]),
-                                in0=by_rows_view(unit[:, first + k, :, b * P : (b + 1) * P]),
-                                in1=by_rows_view(top_halves[b]),
-                                op=ALU.is_equal,
-                            )
-                        if first + k < gpsimd_heads:
-                            nc.gpsimd.tensor_tensor(out=dd[:, k], in0=dd[:, k], in1=g_unit, op=ALU.mult)
-                return dd_groups
+            def product(u, h):
+                c, part = units[u]
+                if h % HEAD_GROUP == 0:
+                    tile = work.tile([P, HEAD_GROUP, UNIT], BF16, align_bytes=64, tag="dd", bufs=2)
+                    dd_tiles[(u, h // HEAD_GROUP)] = tile
+                nc.vector.tensor_tensor(
+                    out=dd_tiles[(u, h // HEAD_GROUP)][:, h % HEAD_GROUP],
+                    in0=words[(u, h)][:].rearrange("p b m u -> p (b m u)").bitcast(BF16),
+                    in1=g_grouped[:, c, part * UNIT : (part + 1) * UNIT],
+                    op=ALU.mult,
+                )
 
-            def multiply_and_quantise(c, part, dd_groups, gpsimd_heads, fillers):
-                g_unit = g_grouped[:, c, part * UNIT : (part + 1) * UNIT]
-                for k, dd in enumerate(dd_groups):
-                    done = max(0, gpsimd_heads - k * HEAD_GROUP)
-                    nc.vector.tensor_tensor(
-                        out=dd[:, done:],
-                        in0=dd[:, done:],
-                        in1=g_unit.unsqueeze(1).to_broadcast([P, HEAD_GROUP - done, UNIT]),
-                        op=ALU.mult,
-                    )
-                for k, dd in enumerate(dd_groups):
-                    heads = slice(k * HEAD_GROUP, (k + 1) * HEAD_GROUP)
-                    nc.vector.quantize_mx(
-                        out=dd_codes[:, c, part, heads].rearrange("p h m -> p (h m)").bitcast(E5M2_X4),
-                        scales=dd_scales[:, c, part, heads].rearrange("p h m -> p (h m)"),
-                        in_=dd[:].rearrange("p h e -> p (h e)"),
-                    )
-                quantise_sn(fillers)
+            def quantise_dd(u, k):
+                c, part = units[u]
+                hs = slice(k * HEAD_GROUP, (k + 1) * HEAD_GROUP)
+                nc.vector.quantize_mx(
+                    out=dd_codes[:, c, part, hs].rearrange("p h m -> p (h m)").bitcast(E5M2_X4),
+                    scales=dd_scales[:, c, part, hs].rearrange("p h m -> p (h m)"),
+                    in_=dd_tiles[(u, k)][:].rearrange("p h e -> p (h e)"),
+                )
 
-            loaded_units = [load_dist_unit(*units[0])]
+            def scale_sn(k, rows):
+                c, h = sn_tiles[k]
+                for j in rows:
+                    nc.vector.tensor_scalar_mul(out=raws[k][:, j], in0=raws[k][:, j], scalar1=inv_s_sb[:, c, j, h : h + 1])
+
+            def regroup_sn(k, half):
+                if half == 0:
+                    tile = work.tile([P, PACK * HEAD_DIM], BF16, align_bytes=64, tag="sn_grouped", bufs=4)
+                    groupeds[k] = tile
+                width = HEAD_DIM // 2
+                nc.scalar.copy(
+                    out=grouped_view(groupeds[k][:, half * PACK * width : (half + 1) * PACK * width]),
+                    in_=by_rows_view(raws[k][:, :, half * width : (half + 1) * width]),
+                )
+
+            def quantise_sn(k):
+                c, h = sn_tiles[k]
+                nc.vector.quantize_mx(
+                    out=sn_codes[:, c, h].bitcast(E4M3_X4), scales=sn_scales[:, c, h], in_=groupeds[k][:]
+                )
+
+            for h in range(HEADS):
+                load_head(0, h)
             nc.sync.dma_start(
                 out=inv_s_sb[:].rearrange("p c j h -> p c (j h)"),
                 in_=inv_s.rearrange("(c p j) h -> p c (j h)", c=PASSES, j=PACK),
             )
-            for c in range(PASSES):
-                g_raw = load_rows(grad_out, c, slice(0, M_ROWS))
-                nc.scalar.copy(out=grouped_view(g_grouped[:, c]), in_=by_rows_view(g_raw[:]))
-            loaded_rows = [load_sn_rows(k) for k in range(SN_PER_UNIT // 2)]
-            loaded_units.append(load_dist_unit(*units[1]))
-            loaded_rows.extend([load_sn_rows(k) for k in range(SN_PER_UNIT // 2, SN_PER_UNIT)])
+            g_raw0 = load_rows(grad_out, 0, slice(0, M_ROWS))
+            load_sn_rows(0)
+            load_head(1, 0)
+            load_head(1, 1)
+            load_sn_rows(1)
+            load_head(1, 2)
+            load_head(1, 3)
+            load_head(1, 4)
+            load_sn_rows(2)
+            load_head(1, 5)
+            load_head(1, 6)
+            load_head(1, 7)
+            g_raw1 = load_rows(grad_out, 1, slice(0, M_ROWS))
             nc.sync.dma_start(out=inv_ro_sb[:], in_=inv_ro.rearrange("(t p) h -> p t h", p=P))
+            regroup_g(0, g_raw0)
 
-            shares = [0] + [GPSIMD_HEADS] * (len(units) - 1)
-            dd_groups = compare(*units[0], loaded_units[0], maximum(loaded_units[0], []), shares[0])
-            waiting = []
-            for u, (c, part) in enumerate(units):
+            for g in range(-HEADS, SLOTS + LAG + 2):
+                u, i = g // HEADS, g % HEADS
                 if u + 1 < len(units):
-                    top_banks = to_psum(maximum(loaded_units[u + 1], waiting[0:2]))
-                else:
-                    quantise_sn(waiting[0:2])
-                multiply_and_quantise(c, part, dd_groups, shares[u], waiting[2:])
-                waiting = []
-                for k in range(u * SN_PER_UNIT, (u + 1) * SN_PER_UNIT):
-                    waiting.append((k, scale_and_regroup_sn(k, loaded_rows[k])))
-                    if k + SN_PER_UNIT < len(sn_tiles):
-                        loaded_rows.append(load_sn_rows(k + SN_PER_UNIT))
-                if u + 2 < len(units):
-                    loaded_units.append(load_dist_unit(*units[u + 2]))
-                elif u + 2 == len(units):
-                    ro_sb = big.tile([P, M_TILES, HEADS * HEAD_DIM], BF16, tag="big")
-                    for t in range(M_TILES):
-                        nc.sync.dma_start(out=ro_sb[:, t], in_=batch_ro[t * P : (t + 1) * P, :])
-                if u + 1 < len(units):
-                    dd_groups = compare(*units[u + 1], loaded_units[u + 1], top_banks, shares[u + 1])
-            quantise_sn(waiting)
+                    maximum_step(u + 1, i)
+                for k, rows in (((g + 3) // 2, (0, 1)), ((g + 2) // 2, (2, 3))):
+                    if g >= 0 and (g + 3 - rows[0] // 2) % 2 == 0 and k < len(sn_tiles):
+                        scale_sn(k, rows)
+                if g == -1:
+                    scale_sn(0, (0, 1, 2, 3))
+                    scale_sn(1, (0, 1))
+                if 0 <= g - LAG < SLOTS:
+                    product((g - LAG) // HEADS, (g - LAG) % HEADS)
+                done = g - LAG - 1
+                if 0 <= done < SLOTS and done % HEAD_GROUP == HEAD_GROUP - 1:
+                    quantise_dd(done // HEADS, (done % HEADS) // HEAD_GROUP)
+                if (g - 3) % 2 == 0 and 0 <= (g - 3) // 2 < len(sn_tiles):
+                    quantise_sn((g - 3) // 2)
+                for b in range(HALVES):
+                    if 0 <= g < SLOTS:
+                        turn_and_subtract(u, i, b)
+                    if 0 <= g - 1 < SLOTS:
+                        turn_back((g - 1) // HEADS, (g - 1) % HEADS, b)
+                if 0 <= g < SLOTS:
+                    for b in range(HALVES):
+                        mask(u, i, b)
+                    regroup_sn(g // 2, g % 2)
+                    if g == 6:
+                        regroup_g(1, g_raw1)
+                if 0 <= g < SLOTS:
+                    if u + 2 < len(units):
+                        load_head(u + 2, i)
+                    elif u + 2 == len(units):
+                        load_ro(i)
+                    if g % 2 == 0 and g // 2 + 3 < len(sn_tiles):
+                        load_sn_rows(g // 2 + 3)
             nc.vector.scalar_tensor_tensor(
                 out=neg_inv_ro_sq[:], in0=inv_ro_sb[:], scalar=-1.0, in1=inv_ro_sb[:], op0=ALU.mult, op1=ALU.mult
             )
@@ -203,7 +260,8 @@ def tile_multiheaddistance_v_kernel(tc, batch_s, batch_ro, dist, inv_s, inv_ro, 
         with tc.tile_pool(name="late", bufs=3) as late, tc.psum_pool(name="psum", bufs=8) as psum:
 
             def ro_of(t, h):
-                return ro_sb[:, t, h * HEAD_DIM : (h + 1) * HEAD_DIM]
+                k = h % RO_HEADS
+                return ro_tiles[t * (HEADS // RO_HEADS) + h // RO_HEADS][:, k * HEAD_DIM : (k + 1) * HEAD_DIM]
 
             def store(t, h, result):
                 nc.sync.dma_start(out=out[t * P : (t + 1) * P, h * HEAD_DIM : (h + 1) * HEAD_DIM], in_=result[:])

@@ -31,6 +31,8 @@ GPSIMD_EVERY = 4
 BIG = 2.0 ** 100
 STREAM_BUFS = 16
 RO_HEADS = 4
+VECTOR_REGROUPS = (13, 15)
+VECTOR_COMPARES = {(3, 6): 27, (3, 7): 28}
 LAG = 2
 
 FLOPS = 2 * HEADS * M_ROWS * N_ROWS * HEAD_DIM
@@ -64,6 +66,7 @@ def tile_multiheaddistance_v_kernel(tc, batch_s, batch_ro, dist, inv_s, inv_ro, 
         units = [(c, part) for c in range(PASSES) for part in range(PARTS)]
         sn_tiles = [(c, h) for c in range(PASSES) for h in range(HEADS)]
         SLOTS = len(units) * HEADS
+        TURNED_SLOTS = SLOTS - len(VECTOR_COMPARES)
 
         heads = {}
         best = {}
@@ -151,16 +154,28 @@ def tile_multiheaddistance_v_kernel(tc, batch_s, batch_ro, dist, inv_s, inv_ro, 
                 for u2 in range(2):
                     nc.tensor.transpose(out=words[(u, h)][:, b, :, u2], in_=pairs[:, u2 * P : (u2 + 1) * P], identity=identity[:])
 
-            def product(u, h):
-                c, part = units[u]
-                if h % HEAD_GROUP == 0:
+            def dd_of(u, h):
+                if (u, h // HEAD_GROUP) not in dd_tiles:
                     tile = work.tile([P, HEAD_GROUP, UNIT], BF16, align_bytes=64, tag="dd", bufs=2)
                     dd_tiles[(u, h // HEAD_GROUP)] = tile
+                return dd_tiles[(u, h // HEAD_GROUP)][:, h % HEAD_GROUP]
+
+            def product(u, h):
+                c, part = units[u]
+                if (u, h) in VECTOR_COMPARES:
+                    factor = dd_of(u, h)
+                else:
+                    factor = words[(u, h)][:].rearrange("p b m u -> p (b m u)").bitcast(BF16)
                 nc.vector.tensor_tensor(
-                    out=dd_tiles[(u, h // HEAD_GROUP)][:, h % HEAD_GROUP],
-                    in0=words[(u, h)][:].rearrange("p b m u -> p (b m u)").bitcast(BF16),
-                    in1=g_grouped[:, c, part * UNIT : (part + 1) * UNIT],
-                    op=ALU.mult,
+                    out=dd_of(u, h), in0=factor, in1=g_grouped[:, c, part * UNIT : (part + 1) * UNIT], op=ALU.mult
+                )
+
+            def compare(u, h):
+                nc.vector.tensor_tensor(
+                    out=grouped_view(dd_of(u, h)),
+                    in0=by_rows_view(heads[(u, h)][:]),
+                    in1=by_rows_view(best[u][:, 0]),
+                    op=ALU.is_equal,
                 )
 
             def quantise_dd(u, k):
@@ -177,15 +192,13 @@ def tile_multiheaddistance_v_kernel(tc, batch_s, batch_ro, dist, inv_s, inv_ro, 
                 for j in rows:
                     nc.vector.tensor_scalar_mul(out=raws[k][:, j], in0=raws[k][:, j], scalar1=inv_s_sb[:, c, j, h : h + 1])
 
-            def regroup_sn(k, half):
-                if half == 0:
-                    tile = work.tile([P, PACK * HEAD_DIM], BF16, align_bytes=64, tag="sn_grouped", bufs=4)
-                    groupeds[k] = tile
-                width = HEAD_DIM // 2
-                nc.scalar.copy(
-                    out=grouped_view(groupeds[k][:, half * PACK * width : (half + 1) * PACK * width]),
-                    in_=by_rows_view(raws[k][:, :, half * width : (half + 1) * width]),
-                )
+            def regroup_sn(k, engine):
+                tile = work.tile([P, PACK * HEAD_DIM], BF16, align_bytes=64, tag="sn_grouped", bufs=4)
+                groupeds[k] = tile
+                if engine == "vector":
+                    nc.vector.tensor_copy(out=grouped_view(tile[:]), in_=by_rows_view(raws[k][:]))
+                else:
+                    nc.scalar.copy(out=grouped_view(tile[:]), in_=by_rows_view(raws[k][:]))
 
             def quantise_sn(k):
                 c, h = sn_tiles[k]
@@ -225,22 +238,31 @@ def tile_multiheaddistance_v_kernel(tc, batch_s, batch_ro, dist, inv_s, inv_ro, 
                 if g == -1:
                     scale_sn(0, (0, 1, 2, 3))
                     scale_sn(1, (0, 1))
-                if 0 <= g - LAG < SLOTS:
+                for (u1, h1), slot in VECTOR_COMPARES.items():
+                    if slot + 1 == g:
+                        product(u1, h1)
+                    if slot == g:
+                        compare(u1, h1)
+                if 0 <= g - LAG < TURNED_SLOTS:
                     product((g - LAG) // HEADS, (g - LAG) % HEADS)
                 done = g - LAG - 1
-                if 0 <= done < SLOTS and done % HEAD_GROUP == HEAD_GROUP - 1:
+                if 0 <= done < TURNED_SLOTS and (done % HEAD_GROUP == HEAD_GROUP - 1 or done == TURNED_SLOTS - 1):
                     quantise_dd(done // HEADS, (done % HEADS) // HEAD_GROUP)
+                if g % 2 == 1 and g // 2 in VECTOR_REGROUPS:
+                    regroup_sn(g // 2, "vector")
                 if (g - 3) % 2 == 0 and 0 <= (g - 3) // 2 < len(sn_tiles):
                     quantise_sn((g - 3) // 2)
                 for b in range(HALVES):
-                    if 0 <= g < SLOTS:
+                    if 0 <= g < TURNED_SLOTS:
                         turn_and_subtract(u, i, b)
-                    if 0 <= g - 1 < SLOTS:
+                    if 0 <= g - 1 < TURNED_SLOTS:
                         turn_back((g - 1) // HEADS, (g - 1) % HEADS, b)
                 if 0 <= g < SLOTS:
                     for b in range(HALVES):
-                        mask(u, i, b)
-                    regroup_sn(g // 2, g % 2)
+                        if g < TURNED_SLOTS:
+                            mask(u, i, b)
+                    if g % 2 == 1 and g // 2 not in VECTOR_REGROUPS:
+                        regroup_sn(g // 2, "scalar")
                     if g == 6:
                         regroup_g(1, g_raw1)
                 if 0 <= g < SLOTS:

@@ -216,35 +216,36 @@ def tile_multiheaddistance_v_kernel(tc, batch_s, batch_ro, dist, inv_s, inv_ro, 
             load_sn_rows(0)
             load_head(1, 0)
             load_head(1, 1)
-            load_sn_rows(1)
             load_head(1, 2)
             load_head(1, 3)
+            load_sn_rows(1)
             load_head(1, 4)
-            load_sn_rows(2)
             load_head(1, 5)
+            load_sn_rows(2)
             load_head(1, 6)
             load_head(1, 7)
+            load_sn_rows(3)
             g_raw1 = load_rows(grad_out, 1, slice(0, M_ROWS))
             nc.sync.dma_start(out=inv_ro_sb[:], in_=inv_ro.rearrange("(t p) h -> p t h", p=P))
             regroup_g(0, g_raw0)
 
             for g in range(-HEADS, SLOTS + LAG + 2):
                 u, i = g // HEADS, g % HEADS
+                if 0 <= g - LAG < TURNED_SLOTS:
+                    product((g - LAG) // HEADS, (g - LAG) % HEADS)
                 if u + 1 < len(units):
                     maximum_step(u + 1, i)
-                for k, rows in (((g + 3) // 2, (0, 1)), ((g + 2) // 2, (2, 3))):
-                    if g >= 0 and (g + 3 - rows[0] // 2) % 2 == 0 and k < len(sn_tiles):
-                        scale_sn(k, rows)
                 if g == -1:
                     scale_sn(0, (0, 1, 2, 3))
-                    scale_sn(1, (0, 1))
+                elif g > 0 and g % 2 == 1 and (g + 1) // 2 < len(sn_tiles):
+                    scale_sn((g + 1) // 2, (0, 1))
+                elif g > 0 and g % 2 == 0 and g // 2 < len(sn_tiles):
+                    scale_sn(g // 2, (2, 3))
                 for (u1, h1), slot in VECTOR_COMPARES.items():
                     if slot + 1 == g:
                         product(u1, h1)
                     if slot == g:
                         compare(u1, h1)
-                if 0 <= g - LAG < TURNED_SLOTS:
-                    product((g - LAG) // HEADS, (g - LAG) % HEADS)
                 done = g - LAG - 1
                 if 0 <= done < TURNED_SLOTS and (done % HEAD_GROUP == HEAD_GROUP - 1 or done == TURNED_SLOTS - 1):
                     quantise_dd(done // HEADS, (done % HEADS) // HEAD_GROUP)
@@ -270,8 +271,8 @@ def tile_multiheaddistance_v_kernel(tc, batch_s, batch_ro, dist, inv_s, inv_ro, 
                         load_head(u + 2, i)
                     elif u + 2 == len(units):
                         load_ro(i)
-                    if g % 2 == 0 and g // 2 + 3 < len(sn_tiles):
-                        load_sn_rows(g // 2 + 3)
+                    if g % 2 == 0 and g // 2 + 4 < len(sn_tiles):
+                        load_sn_rows(g // 2 + 4)
             nc.vector.scalar_tensor_tensor(
                 out=neg_inv_ro_sq[:], in0=inv_ro_sb[:], scalar=-1.0, in1=inv_ro_sb[:], op0=ALU.mult, op1=ALU.mult
             )

@@ -33,6 +33,12 @@ STREAM_BUFS = 16
 RO_HEADS = 4
 VECTOR_REGROUPS = (13, 15)
 VECTOR_COMPARES = {(3, 6): 27, (3, 7): 28}
+MAXIMUM_SLOTS = (
+    (-8, -7, -6, -5, -4, -3, -2, -1),
+    (0, 1, 2, 2, 3, 4, 5, 5),
+    (6, 7, 8, 9, 10, 11, 12, 13),
+    (14, 15, 16, 17, 18, 19, 20, 21),
+)
 LAG = 2
 
 FLOPS = 2 * HEADS * M_ROWS * N_ROWS * HEAD_DIM
@@ -233,8 +239,10 @@ def tile_multiheaddistance_v_kernel(tc, batch_s, batch_ro, dist, inv_s, inv_ro, 
                 u, i = g // HEADS, g % HEADS
                 if 0 <= g - LAG < TURNED_SLOTS:
                     product((g - LAG) // HEADS, (g - LAG) % HEADS)
-                if u + 1 < len(units):
-                    maximum_step(u + 1, i)
+                for u1 in range(len(units)):
+                    for i1 in range(HEADS):
+                        if MAXIMUM_SLOTS[u1][i1] == g:
+                            maximum_step(u1, i1)
                 if g == -1:
                     scale_sn(0, (0, 1, 2, 3))
                 elif g > 0 and g % 2 == 1 and (g + 1) // 2 < len(sn_tiles):

@@ -21,24 +21,47 @@ HEAD_DIM = 512
 PASSES = N_ROWS // K_PASS
 M_TILES = M_ROWS // P
 
-M_PART = 256
-PARTS = M_ROWS // M_PART
-UNIT = PACK * M_PART
-HALVES = M_PART // P
+UNITS = ((0, 0, 128), (0, 128, 128), (0, 256, 256), (1, 0, 256), (1, 256, 256))
+SLOT = 2 * P * PACK
+GROUP = 4
 RUN = 4
-HEAD_GROUP = 4
-GPSIMD_EVERY = 4
 BIG = 2.0 ** 100
 STREAM_BUFS = 16
 RO_HEADS = 4
-VECTOR_REGROUPS = (13, 15)
-VECTOR_COMPARES = {(3, 6): 27, (3, 7): 28}
+SN_HEAD = 1
+HEAD_LOADS = "a a a a g a a a a s b b b b s b b b b s d d s d d s d d s d d s g"
+HEAD_WORK = "m0 m1 g m2 m3 m4 m5 m6 m7 c0 r0"
+VECTOR_COMPARES = {}
 MAXIMUM_SLOTS = (
-    (-8, -7, -6, -5, -4, -3, -2, -1),
-    (0, 1, 2, 2, 3, 4, 5, 5),
-    (6, 7, 8, 9, 10, 11, 12, 13),
+    (0, 0, 1, 1, 1, 2, 2, 2),
+    (3, 3, 4, 4, 5, 5, 6, 6),
+    (7, 8, 9, 10, 11, 12, 13, 13),
     (14, 15, 16, 17, 18, 19, 20, 21),
 )
+FIRST_TILE = 23
+TILE_COUNTS = (1, 1, 1, 1, 1, 1, 1, 1, 1, 1, 1, 3, 3, 3, 3, 3, 3, 3)
+GPSIMD_TILES = (0, 4, 8, 12, 15, 18, 21, 24)
+UNIT3_LOADS = {4: (0, 1), 5: (2, 3), 6: (4, 5), 7: (6, 7)}
+UNIT4_LOADS = {8: 0, 9: 1, 10: 2, 11: 3, 12: 4, 13: 5, 14: 6, 15: 7}
+VECTOR_REGROUPS = ()
+GPSIMD_REGROUPS = ()
+def SN_SLOTS(q):
+    return 2 * q + 1
+
+G1_SLOT = 6
+SN_STEP = 2
+DIFF_BUFS = 3
+MASK_BUFS = 3
+DRN_BUFS = 2
+TURNED_BUFS = 4
+Z_TILES = ()
+Z_LAG = 0
+GROUPED_BUFS = 5
+HEAD_Q_SLOT = 1
+B2_TILES = tuple(range(16, 32))
+TILES_LAST = False
+PRODUCT_LATE = 0
+TB_LAG = 1
 LAG = 2
 
 FLOPS = 2 * HEADS * M_ROWS * N_ROWS * HEAD_DIM
@@ -55,9 +78,11 @@ def grouped_view(ap):
 def tile_multiheaddistance_v_kernel(tc, batch_s, batch_ro, dist, inv_s, inv_ro, grad_out, out):
     nc = tc.nc
 
-    with tc.tile_pool(name="keep", bufs=1) as keep, tc.tile_pool(name="stream", bufs=STREAM_BUFS) as stream:
-        dd_codes = keep.tile([P, PASSES, PARTS, HEADS, M_PART], U32, align_bytes=64)
-        dd_scales = keep.tile([P, PASSES, PARTS, HEADS, M_PART], U8, align_bytes=64)
+    with tc.tile_pool(name="keep", bufs=1) as keep, tc.tile_pool(name="stream", bufs=STREAM_BUFS) as stream, tc.tile_pool(
+        name="rows", bufs=6
+    ) as rows_pool, tc.tile_pool(name="work", bufs=1) as work, tc.psum_pool(name="psum", bufs=1) as psum, tc.manual_schedule():
+        dd_codes = keep.tile([P, HEADS, SLOT], U32, align_bytes=64)
+        dd_scales = keep.tile([P, HEADS, SLOT], U8, align_bytes=64)
         sn_codes = keep.tile([P, PASSES, HEADS, HEAD_DIM], U32, align_bytes=64)
         sn_scales = keep.tile([P, PASSES, HEADS, HEAD_DIM], U8, align_bytes=64)
         inv_s_sb = keep.tile([P, PASSES, PACK, HEADS], F32)
@@ -69,10 +94,14 @@ def tile_multiheaddistance_v_kernel(tc, batch_s, batch_ro, dist, inv_s, inv_ro, 
         identity = keep.tile([P, P], F32)
         make_identity(nc, identity[:])
 
-        units = [(c, part) for c in range(PASSES) for part in range(PARTS)]
-        sn_tiles = [(c, h) for c in range(PASSES) for h in range(HEADS)]
-        SLOTS = len(units) * HEADS
+        slots = []
+        for u, (c, m0, width) in enumerate(UNITS):
+            pairs = [(h, b) for h in range(HEADS) for b in range(width // P)]
+            slots += [(u, pairs[k : k + 2]) for k in range(0, len(pairs), 2)]
+        sn_tiles = [(c, h) for h in range(HEADS) for c in range(PASSES)]
+        SLOTS = len(slots)
         TURNED_SLOTS = SLOTS - len(VECTOR_COMPARES)
+        tiles = [(t, h) for part in range(2) for h in range(HEADS) for t in (2 * part, 2 * part + 1)]
 
         heads = {}
         best = {}
@@ -82,286 +111,416 @@ def tile_multiheaddistance_v_kernel(tc, batch_s, batch_ro, dist, inv_s, inv_ro, 
         words = {}
         dd_tiles = {}
         raws = {}
+        g_raws = {}
         groupeds = {}
         ro_tiles = []
+        drns = {}
+        results = {}
+        ys = {}
 
-        with tc.tile_pool(name="rows", bufs=6) as rows_pool, tc.tile_pool(
-            name="work", bufs=1
-        ) as work, tc.psum_pool(name="turn", bufs=4) as turn, tc.manual_schedule():
+        def load_head(u, h):
+            c, m0, width = UNITS[u]
+            if u == 1:
+                tile = heads[(0, h)][0]
+            else:
+                tile = stream.tile([P, PACK * 256], F32, tag="stream")
+            first = PACK * P if u == 1 else 0
+            view = tile[:, first : first + PACK * width].rearrange("p (j m) -> p j m", j=PACK)
+            rows = dist[h, c * K_PASS : (c + 1) * K_PASS, m0 : m0 + width]
+            nc.sync.dma_start(out=view, in_=rows.rearrange("(p j) m -> p j m", j=PACK))
+            heads[(u, h)] = (tile, view)
 
-            def load_head(u, h):
-                c, part = units[u]
-                tile = stream.tile([P, PACK, M_PART], F32, tag="stream")
-                rows = dist[h, c * K_PASS : (c + 1) * K_PASS, part * M_PART : (part + 1) * M_PART]
-                nc.sync.dma_start(out=tile[:], in_=rows.rearrange("(p j) m -> p j m", j=PACK))
-                heads[(u, h)] = tile
+        def head(u, h):
+            return heads[(u, h)][1]
 
-            def load_rows(src, c, columns):
-                raw = rows_pool.tile([P, PACK, HEAD_DIM], BF16, tag="raw")
-                nc.sync.dma_start(
-                    out=raw[:], in_=src[c * K_PASS : (c + 1) * K_PASS, columns].rearrange("(p j) w -> p j w", j=PACK)
-                )
-                return raw
-
-            def load_sn_rows(k):
-                c, h = sn_tiles[k]
-                raws[k] = load_rows(batch_s, c, slice(h * HEAD_DIM, (h + 1) * HEAD_DIM))
-
-            def load_ro(k):
-                t, half = k // (HEADS // RO_HEADS), k % (HEADS // RO_HEADS)
-                tile = stream.tile([P, RO_HEADS * HEAD_DIM], BF16, tag="stream")
-                width = RO_HEADS * HEAD_DIM
-                nc.sync.dma_start(out=tile[:], in_=batch_ro[t * P : (t + 1) * P, half * width : (half + 1) * width])
-                ro_tiles.append(tile)
-
-            def regroup_g(c, g_raw):
-                nc.scalar.copy(out=grouped_view(g_grouped[:, c]), in_=by_rows_view(g_raw[:]))
-
-            def maximum_step(u, i):
-                if i == 0:
-                    tile = work.tile([P, 2, PACK, M_PART], F32, tag="best")
-                    best[u] = tile
-                b = best[u]
-                if i < 2:
-                    nc.vector.tensor_tensor(out=b[:, i], in0=heads[(u, 2 * i)][:], in1=heads[(u, 2 * i + 1)][:], op=ALU.max)
-                elif i < 6:
-                    nc.vector.tensor_tensor(out=b[:, i % 2], in0=b[:, i % 2], in1=heads[(u, i + 2)][:], op=ALU.max)
-                elif i == 6:
-                    nc.vector.tensor_tensor(out=b[:, 0], in0=b[:, 0], in1=b[:, 1], op=ALU.max)
-                else:
-                    tile = work.tile([P, PACK, M_PART], F32, tag="minus_top", bufs=2)
-                    nc.vector.tensor_scalar_mul(out=tile[:], in0=b[:, 0], scalar1=-1.0)
-                    minus_top[u] = tile
-
-            def turn_and_subtract(u, h, b):
-                cols = slice(b * P, (b + 1) * P)
-                diff = turn.tile([P, PACK, P], F32, tag="diff")
-                for j in range(PACK):
-                    nc.tensor.matmul(
-                        out=diff[:, j], lhsT=heads[(u, h)][:, j, cols], rhs=identity[:], is_transpose=True, start=True, stop=False
-                    )
-                    nc.tensor.matmul(
-                        out=diff[:, j], lhsT=minus_top[u][:, j, cols], rhs=identity[:], is_transpose=True, start=False, stop=True
-                    )
-                diffs[(u, h, b)] = diff
-
-            def mask(u, h, b):
-                tile = work.tile([P, 2, P, 2], BF16, tag="turned", bufs=4)
-                nc.scalar.activation(
-                    out=tile[:], in_=diffs[(u, h, b)][:].rearrange("m (u e) p -> m u p e", e=2), func=RELU, scale=BIG, bias=1.0
-                )
-                turned[(u, h, b)] = tile
-
-            def turn_back(u, h, b):
-                if b == 0:
-                    tile = turn.tile([P, HALVES, P, 2], F32, tag="mask")
-                    words[(u, h)] = tile
-                pairs = turned[(u, h, b)][:].rearrange("m u p e -> m (u p e)").bitcast(F32)
-                for u2 in range(2):
-                    nc.tensor.transpose(out=words[(u, h)][:, b, :, u2], in_=pairs[:, u2 * P : (u2 + 1) * P], identity=identity[:])
-
-            def dd_of(u, h):
-                if (u, h // HEAD_GROUP) not in dd_tiles:
-                    tile = work.tile([P, HEAD_GROUP, UNIT], BF16, align_bytes=64, tag="dd", bufs=2)
-                    dd_tiles[(u, h // HEAD_GROUP)] = tile
-                return dd_tiles[(u, h // HEAD_GROUP)][:, h % HEAD_GROUP]
-
-            def product(u, h):
-                c, part = units[u]
-                if (u, h) in VECTOR_COMPARES:
-                    factor = dd_of(u, h)
-                else:
-                    factor = words[(u, h)][:].rearrange("p b m u -> p (b m u)").bitcast(BF16)
-                nc.vector.tensor_tensor(
-                    out=dd_of(u, h), in0=factor, in1=g_grouped[:, c, part * UNIT : (part + 1) * UNIT], op=ALU.mult
-                )
-
-            def compare(u, h):
-                nc.vector.tensor_tensor(
-                    out=grouped_view(dd_of(u, h)),
-                    in0=by_rows_view(heads[(u, h)][:]),
-                    in1=by_rows_view(best[u][:, 0]),
-                    op=ALU.is_equal,
-                )
-
-            def quantise_dd(u, k):
-                c, part = units[u]
-                hs = slice(k * HEAD_GROUP, (k + 1) * HEAD_GROUP)
-                nc.vector.quantize_mx(
-                    out=dd_codes[:, c, part, hs].rearrange("p h m -> p (h m)").bitcast(E5M2_X4),
-                    scales=dd_scales[:, c, part, hs].rearrange("p h m -> p (h m)"),
-                    in_=dd_tiles[(u, k)][:].rearrange("p h e -> p (h e)"),
-                )
-
-            def scale_sn(k, rows):
-                c, h = sn_tiles[k]
-                for j in rows:
-                    nc.vector.tensor_scalar_mul(out=raws[k][:, j], in0=raws[k][:, j], scalar1=inv_s_sb[:, c, j, h : h + 1])
-
-            def regroup_sn(k, engine):
-                tile = work.tile([P, PACK * HEAD_DIM], BF16, align_bytes=64, tag="sn_grouped", bufs=4)
-                groupeds[k] = tile
-                if engine == "vector":
-                    nc.vector.tensor_copy(out=grouped_view(tile[:]), in_=by_rows_view(raws[k][:]))
-                else:
-                    nc.scalar.copy(out=grouped_view(tile[:]), in_=by_rows_view(raws[k][:]))
-
-            def quantise_sn(k):
-                c, h = sn_tiles[k]
-                nc.vector.quantize_mx(
-                    out=sn_codes[:, c, h].bitcast(E4M3_X4), scales=sn_scales[:, c, h], in_=groupeds[k][:]
-                )
-
-            for h in range(HEADS):
-                load_head(0, h)
+        def load_rows(src, c, columns):
+            raw = rows_pool.tile([P, PACK, HEAD_DIM], BF16, tag="raw")
             nc.sync.dma_start(
-                out=inv_s_sb[:].rearrange("p c j h -> p c (j h)"),
-                in_=inv_s.rearrange("(c p j) h -> p c (j h)", c=PASSES, j=PACK),
+                out=raw[:], in_=src[c * K_PASS : (c + 1) * K_PASS, columns].rearrange("(p j) w -> p j w", j=PACK)
             )
-            g_raw0 = load_rows(grad_out, 0, slice(0, M_ROWS))
-            load_sn_rows(0)
-            load_head(1, 0)
-            load_head(1, 1)
-            load_head(1, 2)
-            load_head(1, 3)
-            load_sn_rows(1)
-            load_head(1, 4)
-            load_head(1, 5)
-            load_sn_rows(2)
-            load_head(1, 6)
-            load_head(1, 7)
-            load_sn_rows(3)
-            g_raw1 = load_rows(grad_out, 1, slice(0, M_ROWS))
-            nc.sync.dma_start(out=inv_ro_sb[:], in_=inv_ro.rearrange("(t p) h -> p t h", p=P))
-            regroup_g(0, g_raw0)
+            return raw
 
-            for g in range(-HEADS, SLOTS + LAG + 2):
-                u, i = g // HEADS, g % HEADS
-                if 0 <= g - LAG < TURNED_SLOTS:
-                    product((g - LAG) // HEADS, (g - LAG) % HEADS)
-                for u1 in range(len(units)):
-                    for i1 in range(HEADS):
-                        if MAXIMUM_SLOTS[u1][i1] == g:
-                            maximum_step(u1, i1)
-                if g == -1:
-                    scale_sn(0, (0, 1, 2, 3))
-                elif g > 0 and g % 2 == 1 and (g + 1) // 2 < len(sn_tiles):
-                    scale_sn((g + 1) // 2, (0, 1))
-                elif g > 0 and g % 2 == 0 and g // 2 < len(sn_tiles):
-                    scale_sn(g // 2, (2, 3))
-                for (u1, h1), slot in VECTOR_COMPARES.items():
-                    if slot + 1 == g:
-                        product(u1, h1)
-                    if slot == g:
-                        compare(u1, h1)
-                done = g - LAG - 1
-                if 0 <= done < TURNED_SLOTS and (done % HEAD_GROUP == HEAD_GROUP - 1 or done == TURNED_SLOTS - 1):
-                    quantise_dd(done // HEADS, (done % HEADS) // HEAD_GROUP)
-                if g % 2 == 1 and g // 2 in VECTOR_REGROUPS:
-                    regroup_sn(g // 2, "vector")
-                if (g - 3) % 2 == 0 and 0 <= (g - 3) // 2 < len(sn_tiles):
-                    quantise_sn((g - 3) // 2)
-                for b in range(HALVES):
-                    if 0 <= g < TURNED_SLOTS:
-                        turn_and_subtract(u, i, b)
-                    if 0 <= g - 1 < TURNED_SLOTS:
-                        turn_back((g - 1) // HEADS, (g - 1) % HEADS, b)
-                if 0 <= g < SLOTS:
-                    for b in range(HALVES):
-                        if g < TURNED_SLOTS:
-                            mask(u, i, b)
-                    if g % 2 == 1 and g // 2 not in VECTOR_REGROUPS:
-                        regroup_sn(g // 2, "scalar")
-                    if g == 6:
-                        regroup_g(1, g_raw1)
-                if 0 <= g < SLOTS:
-                    if u + 2 < len(units):
-                        load_head(u + 2, i)
-                    elif u + 2 == len(units):
-                        load_ro(i)
-                    if g % 2 == 0 and g // 2 + 4 < len(sn_tiles):
-                        load_sn_rows(g // 2 + 4)
-            nc.vector.scalar_tensor_tensor(
-                out=neg_inv_ro_sq[:], in0=inv_ro_sb[:], scalar=-1.0, in1=inv_ro_sb[:], op0=ALU.mult, op1=ALU.mult
-            )
+        def load_sn_rows(k):
+            c, h = sn_tiles[k]
+            raws[k] = load_rows(batch_s, c, slice(h * HEAD_DIM, (h + 1) * HEAD_DIM))
 
-        tiles = [(t, h) for t in range(M_TILES) for h in range(HEADS)]
-        groups = [tiles[k : k + GPSIMD_EVERY] for k in range(0, len(tiles), GPSIMD_EVERY)]
+        def load_g(c):
+            g_raws[c] = load_rows(grad_out, c, slice(0, M_ROWS))
 
-        with tc.tile_pool(name="late", bufs=3) as late, tc.psum_pool(name="psum", bufs=8) as psum:
+        def load_ro(k):
+            t, half = k // (HEADS // RO_HEADS), k % (HEADS // RO_HEADS)
+            tile = stream.tile([P, RO_HEADS * HEAD_DIM], BF16, tag="stream")
+            width = RO_HEADS * HEAD_DIM
+            nc.sync.dma_start(out=tile[:], in_=batch_ro[t * P : (t + 1) * P, half * width : (half + 1) * width])
+            ro_tiles.append(tile)
 
-            def ro_of(t, h):
-                k = h % RO_HEADS
-                return ro_tiles[t * (HEADS // RO_HEADS) + h // RO_HEADS][:, k * HEAD_DIM : (k + 1) * HEAD_DIM]
+        def regroup_g(c):
+            nc.scalar.copy(out=grouped_view(g_grouped[:, c]), in_=by_rows_view(g_raws[c][:]))
 
-            def store(t, h, result):
-                nc.sync.dma_start(out=out[t * P : (t + 1) * P, h * HEAD_DIM : (h + 1) * HEAD_DIM], in_=result[:])
+        def maximum_step(u, i):
+            width = UNITS[u][2]
+            if i == 0:
+                tile = work.tile([P, 2, PACK, width], F32, tag="best")
+                best[u] = tile
+            b = best[u]
+            if i < 2:
+                nc.vector.tensor_tensor(out=b[:, i], in0=head(u, 2 * i), in1=head(u, 2 * i + 1), op=ALU.max)
+            elif i < 6:
+                nc.vector.tensor_tensor(out=b[:, i % 2], in0=b[:, i % 2], in1=head(u, i + 2), op=ALU.max)
+            elif i == 6:
+                nc.vector.tensor_tensor(out=b[:, 0], in0=b[:, 0], in1=b[:, 1], op=ALU.max)
+            else:
+                tile = work.tile([P, PACK, width], F32, tag="minus_top", bufs=2)
+                nc.vector.tensor_scalar_mul(out=tile[:], in0=b[:, 0], scalar1=-1.0)
+                minus_top[u] = tile
 
-            def multiply(t, h):
-                part, m_cols = t // 2, slice((t % 2) * P, (t % 2 + 1) * P)
-                drn = psum.tile([P, HEAD_DIM], F32, tag="drn")
-                for c in range(PASSES):
-                    nc.tensor.matmul_mx(
-                        out=drn[:],
-                        lhsT=dd_codes[:, c, part, h, m_cols].bitcast(E5M2_X4),
-                        lhsT_scale=dd_scales[:, c, part, h, m_cols],
-                        rhs=sn_codes[:, c, h].bitcast(E4M3_X4),
-                        rhs_scale=sn_scales[:, c, h],
-                        start=(c == 0),
-                        stop=(c == PASSES - 1),
-                    )
-                return drn
-
-            def first_half(group):
-                drns = [multiply(t, h) for t, h in group]
-                t, h = group[0]
-                y = late.tile([P, HEAD_DIM], F32, tag="y")
-                nc.scalar.activation(out=y[:], in_=drns[0][:], func=COPY, scale=inv_ro_sb[:, t, h : h + 1])
-                products = late.tile([P, HEAD_DIM], F32, tag="products_g")
-                nc.gpsimd.tensor_tensor(out=products[:], in0=y[:], in1=ro_of(t, h), op=ALU.mult)
-                for (t, h), drn in zip(group[1:], drns[1:]):
-                    unused = late.tile([P, HEAD_DIM], F32, tag="products_v")
-                    nc.vector.scalar_tensor_tensor(
-                        out=unused[:],
-                        in0=drn[:],
-                        scalar=neg_inv_ro_sq[:, t, h : h + 1],
-                        in1=ro_of(t, h),
-                        op0=ALU.mult,
-                        op1=ALU.mult,
-                        accum_out=coef_v[:, t, h : h + 1],
-                    )
-                results = []
-                for (t, h), drn in zip(group[1:], drns[1:]):
-                    result = late.tile([P, HEAD_DIM], F32, tag="result_v", bufs=3 * GPSIMD_EVERY)
-                    nc.vector.scalar_tensor_tensor(
-                        out=result[:], in0=ro_of(t, h), scalar=coef_v[:, t, h : h + 1], in1=drn[:], op0=ALU.mult, op1=ALU.add
-                    )
-                    results.append(result)
-                return y, products, results
-
-            def second_half(group, y, products, results):
-                t, h = group[0]
-                nc.scalar.activation(
-                    out=products[:],
-                    in_=products[:],
-                    func=COPY,
-                    scale=neg_inv_ro_sq[:, t, h : h + 1],
-                    accum_out=coef_g[:, t, h : h + 1],
+        def turn_and_subtract(g, k):
+            u, pairs = slots[g]
+            h, b = pairs[k]
+            cols = slice(b * P, (b + 1) * P)
+            diff = psum.tile([P, PACK, P], F32, tag="diff", bufs=DIFF_BUFS)
+            for j in range(PACK):
+                nc.tensor.matmul(
+                    out=diff[:, j], lhsT=head(u, h)[:, j, cols], rhs=identity[:], is_transpose=True, start=True, stop=False
                 )
-                result = late.tile([P, HEAD_DIM], F32, tag="result_g")
+                nc.tensor.matmul(
+                    out=diff[:, j], lhsT=minus_top[u][:, j, cols], rhs=identity[:], is_transpose=True, start=False, stop=True
+                )
+            diffs[(g, k)] = diff
+
+        def mask(g, k):
+            tile = work.tile([P, 2, P, 2], BF16, tag="turned", bufs=TURNED_BUFS)
+            nc.scalar.activation(
+                out=tile[:], in_=diffs[(g, k)][:].rearrange("m (u e) p -> m u p e", e=2), func=RELU, scale=BIG, bias=1.0
+            )
+            turned[(g, k)] = tile
+
+        def turn_back(g, k):
+            if k == 0:
+                tile = psum.tile([P, 2, P, 2], F32, tag="mask", bufs=MASK_BUFS)
+                words[g] = tile
+            rows = turned[(g, k)][:].rearrange("m u p e -> m (u p e)").bitcast(F32)
+            for u2 in range(2):
+                nc.tensor.transpose(out=words[g][:, k, :, u2], in_=rows[:, u2 * P : (u2 + 1) * P], identity=identity[:])
+
+        def dd_of(g):
+            if g // GROUP not in dd_tiles:
+                tile = work.tile([P, GROUP, SLOT], BF16, align_bytes=64, tag="dd", bufs=2)
+                dd_tiles[g // GROUP] = tile
+            return dd_tiles[g // GROUP][:, g % GROUP]
+
+        def product(g):
+            u, pairs = slots[g]
+            c, m0, width = UNITS[u]
+            if g in VECTOR_COMPARES:
+                factor = dd_of(g)
+            else:
+                factor = words[g][:].rearrange("p b m u -> p (b m u)").bitcast(BF16)
+            n = min(width * PACK, SLOT)
+            for first in range(0, SLOT, n):
+                nc.vector.tensor_tensor(
+                    out=dd_of(g)[:, first : first + n],
+                    in0=factor[:, first : first + n],
+                    in1=g_grouped[:, c, m0 * PACK : m0 * PACK + n],
+                    op=ALU.mult,
+                )
+
+        def compare(g):
+            u, pairs = slots[g]
+            nc.vector.tensor_tensor(
+                out=grouped_view(dd_of(g)),
+                in0=by_rows_view(head(u, pairs[0][0])),
+                in1=by_rows_view(best[u][:, 0]),
+                op=ALU.is_equal,
+            )
+
+        def quantise_dd(k):
+            nc.vector.quantize_mx(
+                out=dd_codes[:, k].bitcast(E5M2_X4),
+                scales=dd_scales[:, k],
+                in_=dd_tiles[k][:].rearrange("p h e -> p (h e)"),
+            )
+
+        def dd_columns(c, t, h):
+            for g, (u, pairs) in enumerate(slots):
+                for k, (h2, b) in enumerate(pairs):
+                    if UNITS[u][0] == c and UNITS[u][1] + b * P == t * P and h2 == h:
+                        first = (g % GROUP) * 2 * P + k * P
+                        return g // GROUP, slice(first, first + P)
+
+        def scale_sn(k, rows):
+            c, h = sn_tiles[k]
+            for j in rows:
+                nc.vector.tensor_scalar_mul(out=raws[k][:, j], in0=raws[k][:, j], scalar1=inv_s_sb[:, c, j, h : h + 1])
+
+        def regroup_sn(k, engine=None):
+            tile = work.tile([P, PACK * HEAD_DIM], BF16, align_bytes=64, tag="sn_grouped", bufs=GROUPED_BUFS)
+            groupeds[k] = tile
+            if k in GPSIMD_REGROUPS:
                 nc.gpsimd.tensor_scalar(
-                    out=result[:], in0=ro_of(t, h), scalar1=coef_g[:, t, h : h + 1], scalar2=0.0, op0=ALU.mult, op1=ALU.add
+                    out=tile[:].rearrange("p (d j) -> p d j", j=PACK),
+                    in0=raws[k][:].rearrange("p j d -> p d j"),
+                    scalar1=1.0,
+                    scalar2=0.0,
+                    op0=ALU.mult,
+                    op1=ALU.add,
                 )
-                nc.gpsimd.tensor_tensor(out=result[:], in0=result[:], in1=y[:], op=ALU.add)
-                for (t, h), result_v in zip(group[1:], results):
-                    nc.scalar.activation(out=result_v[:], in_=result_v[:], func=COPY, scale=inv_ro_sb[:, t, h : h + 1])
-                    store(t, h, result_v)
-                store(group[0][0], group[0][1], result)
+            elif k in VECTOR_REGROUPS:
+                nc.vector.tensor_copy(out=grouped_view(tile[:]), in_=by_rows_view(raws[k][:]))
+            else:
+                nc.scalar.copy(out=grouped_view(tile[:]), in_=by_rows_view(raws[k][:]))
 
-            with tc.manual_schedule():
-                halfway = first_half(groups[0])
-                for k in range(1, len(groups)):
-                    ahead = first_half(groups[k])
-                    second_half(groups[k - 1], *halfway)
-                    halfway = ahead
-                second_half(groups[-1], *halfway)
+        def quantise_sn(k):
+            c, h = sn_tiles[k]
+            nc.vector.quantize_mx(out=sn_codes[:, c, h].bitcast(E4M3_X4), scales=sn_scales[:, c, h], in_=groupeds[k][:])
+
+        def ro_of(t, h):
+            k = h % RO_HEADS
+            return ro_tiles[t * (HEADS // RO_HEADS) + h // RO_HEADS][:, k * HEAD_DIM : (k + 1) * HEAD_DIM]
+
+        def store(t, h, result):
+            nc.sync.dma_start(out=out[t * P : (t + 1) * P, h * HEAD_DIM : (h + 1) * HEAD_DIM], in_=result)
+
+        def multiply(x, tag, bufs):
+            t, h = tiles[x]
+            drn = psum.tile([P, HEAD_DIM], F32, tag=tag, bufs=bufs)
+            for c in range(PASSES):
+                group, columns = dd_columns(c, t, h)
+                nc.tensor.matmul_mx(
+                    out=drn[:],
+                    lhsT=dd_codes[:, group, columns].bitcast(E5M2_X4),
+                    lhsT_scale=dd_scales[:, group, columns],
+                    rhs=sn_codes[:, c, h].bitcast(E4M3_X4),
+                    rhs_scale=sn_scales[:, c, h],
+                    start=(c == 0),
+                    stop=(c == PASSES - 1),
+                )
+            drns[x] = drn
+
+        def vector_sum(x):
+            t, h = tiles[x]
+            unused = work.tile([P, HEAD_DIM], BF16, tag="unused", bufs=1)
+            nc.vector.scalar_tensor_tensor(
+                out=unused[:],
+                in0=drns[x][:],
+                scalar=neg_inv_ro_sq[:, t, h : h + 1],
+                in1=ro_of(t, h),
+                op0=ALU.mult,
+                op1=ALU.mult,
+                accum_out=coef_v[:, t, h : h + 1],
+            )
+
+        def vector_difference(x):
+            t, h = tiles[x]
+            if x in late_results:
+                result = stream.tile([P, HEAD_DIM], F32, tag="stream")
+            else:
+                result = rows_pool.tile([P, HEAD_DIM], F32, tag="raw")
+            nc.vector.scalar_tensor_tensor(
+                out=result[:], in0=ro_of(t, h), scalar=coef_v[:, t, h : h + 1], in1=drns[x][:], op0=ALU.mult, op1=ALU.add
+            )
+            results[x] = result
+
+        def last_factor(x):
+            t, h = tiles[x]
+            nc.scalar.activation(out=results[x][:], in_=results[x][:], func=COPY, scale=inv_ro_sb[:, t, h : h + 1])
+            store(t, h, results[x][:])
+
+        def gpsimd_y(x):
+            t, h = tiles[x]
+            y = work.tile([P, 2, HEAD_DIM], F32, align_bytes=64, tag="sn_grouped", bufs=GROUPED_BUFS)
+            nc.scalar.activation(out=y[:, 0], in_=drns[x][:], func=COPY, scale=inv_ro_sb[:, t, h : h + 1])
+            ys[x] = y
+
+        def gpsimd_products(x):
+            nc.gpsimd.tensor_tensor(out=ys[x][:, 1], in0=ys[x][:, 0], in1=ro_of(*tiles[x]), op=ALU.mult)
+
+        def gpsimd_sum(x):
+            t, h = tiles[x]
+            nc.scalar.activation(
+                out=ys[x][:, 1],
+                in_=ys[x][:, 1],
+                func=COPY,
+                scale=neg_inv_ro_sq[:, t, h : h + 1],
+                accum_out=coef_g[:, t, h : h + 1],
+            )
+
+        def gpsimd_difference(x):
+            t, h = tiles[x]
+            if x in B2_TILES:
+                nc.scalar.activation(out=ys[x][:, 1], in_=ro_of(t, h), func=COPY, scale=coef_g[:, t, h : h + 1])
+            else:
+                nc.gpsimd.tensor_scalar(
+                    out=ys[x][:, 1], in0=ro_of(t, h), scalar1=coef_g[:, t, h : h + 1], scalar2=0.0, op0=ALU.mult, op1=ALU.add
+                )
+            nc.gpsimd.tensor_tensor(out=ys[x][:, 1], in0=ys[x][:, 1], in1=ys[x][:, 0], op=ALU.add)
+
+        def gpsimd_z(x):
+            t, h = tiles[x]
+            z = work.tile([P, HEAD_DIM], F32, align_bytes=64, tag="z", bufs=2)
+            nc.gpsimd.tensor_scalar(out=z[:], in0=ro_of(t, h), scalar1=coef_v[:, t, h : h + 1], scalar2=0.0, op0=ALU.mult, op1=ALU.add)
+            ys[x] = z
+
+        def z_difference(x):
+            t, h = tiles[x]
+            if x in late_results:
+                result = stream.tile([P, HEAD_DIM], F32, tag="stream")
+            else:
+                result = rows_pool.tile([P, HEAD_DIM], F32, tag="raw")
+            nc.vector.scalar_tensor_tensor(
+                out=result[:], in0=drns[x][:], scalar=inv_ro_sb[:, t, h : h + 1], in1=ys[x][:], op0=ALU.mult, op1=ALU.add
+            )
+            store(t, h, result[:])
+
+        nc.sync.dma_start(
+            out=inv_s_sb[:].rearrange("p c j h -> p c (j h)"),
+            in_=inv_s.rearrange("(c p j) h -> p c (j h)", c=PASSES, j=PACK),
+        )
+        n_s, n_g = 0, 0
+        n_u = {"a": 0, "b": 0, "d": 0}
+        for what in HEAD_LOADS.split():
+            if what == "s":
+                load_sn_rows(n_s)
+                n_s += 1
+            elif what in n_u:
+                load_head("abd".index(what), n_u[what])
+                n_u[what] += 1
+            elif what == "g":
+                load_g(n_g)
+                n_g += 1
+        nc.sync.dma_start(out=inv_ro_sb[:], in_=inv_ro.rearrange("(t p) h -> p t h", p=P))
+
+        all_rows = range(PACK)
+        for what in HEAD_WORK.split():
+            if what[0] == "c":
+                scale_sn(int(what[1:]), all_rows)
+            elif what[0] == "r":
+                regroup_sn(int(what[1:]))
+            elif what[0] == "q":
+                quantise_sn(int(what[1:]))
+            elif what[0] == "m":
+                maximum_step(0, int(what[1:]))
+            else:
+                regroup_g(0)
+        head_q = [int(w[1:]) for w in HEAD_WORK.split() if w[0] == "q"]
+        head_r = [int(w[1:]) for w in HEAD_WORK.split() if w[0] == "r"]
+
+        tile_slots = {}
+        x = 0
+        for k, count in enumerate(TILE_COUNTS):
+            tile_slots[FIRST_TILE + k] = [y for y in range(x, x + count) if y < len(tiles)]
+            x += count
+        last_slot = FIRST_TILE + len(TILE_COUNTS) + 3
+
+        regroup_slot = {SN_HEAD + q: SN_SLOTS(q) for q in range(len(sn_tiles) - SN_HEAD)}
+        next_tag = 0
+
+        pending = []
+        diff_slot = {}
+        late_results = [x for x in range(len(tiles)) if x not in GPSIMD_TILES][-8:]
+
+        def vector_tiles(g):
+            for x in tile_slots.get(g - 1, []):
+                if x not in GPSIMD_TILES:
+                    vector_sum(x)
+                    if x in Z_TILES:
+                        gpsimd_z(x)
+                    if pending:
+                        finish(pending.pop(), g)
+                    pending.append(x)
+            if pending and not any(x not in GPSIMD_TILES for x in tile_slots.get(g - 1, [])) and (g > FIRST_TILE + 1):
+                finish(pending.pop(), g)
+
+        def finish(y, g):
+            if y in Z_TILES:
+                z_difference(y)
+            else:
+                vector_difference(y)
+                diff_slot.setdefault(g, []).append(y)
+
+        for g in range(last_slot + 1):
+            if not (PRODUCT_LATE and g >= PRODUCT_LATE) and 0 <= g - LAG < TURNED_SLOTS:
+                product(g - LAG)
+            if not TILES_LAST:
+                vector_tiles(g)
+            for u1 in range(1, len(UNITS)):
+                for i1 in range(HEADS):
+                    if MAXIMUM_SLOTS[u1 - 1][i1] == g:
+                        maximum_step(u1, i1)
+            for k, slot in regroup_slot.items():
+                if slot - 1 == g and slot - 2 < 0:
+                    scale_sn(k, all_rows)
+                elif slot - 2 == g:
+                    scale_sn(k, (0, 1))
+                elif slot - 1 == g:
+                    scale_sn(k, (2, 3))
+            for slot1, slot in VECTOR_COMPARES.items():
+                if slot + 1 == g:
+                    product(slot1)
+                if slot == g:
+                    compare(slot1)
+            done = g - LAG - 1
+            if 0 <= done < TURNED_SLOTS and (done % GROUP == GROUP - 1 or done == TURNED_SLOTS - 1):
+                quantise_dd(done // GROUP)
+            if g == HEAD_Q_SLOT:
+                for k in head_r:
+                    if k not in head_q:
+                        quantise_sn(k)
+            for k, slot in regroup_slot.items():
+                if slot == g and k in VECTOR_REGROUPS:
+                    regroup_sn(k)
+                if slot + 2 == g:
+                    quantise_sn(k)
+            if g == FIRST_TILE - 2:
+                nc.vector.scalar_tensor_tensor(
+                    out=neg_inv_ro_sq[:], in0=inv_ro_sb[:], scalar=-1.0, in1=inv_ro_sb[:], op0=ALU.mult, op1=ALU.mult
+                )
+            if PRODUCT_LATE and g >= PRODUCT_LATE and 0 <= g - LAG < TURNED_SLOTS:
+                product(g - LAG)
+            if TILES_LAST:
+                vector_tiles(g)
+            for k in range(2):
+                if 0 <= g < TURNED_SLOTS:
+                    turn_and_subtract(g, k)
+                if 0 <= g - TB_LAG < TURNED_SLOTS:
+                    turn_back(g - TB_LAG, k)
+            for x in tile_slots.get(g - 1, []):
+                if x in GPSIMD_TILES:
+                    gpsimd_y(x)
+                    gpsimd_products(x)
+            for x in diff_slot.get(g - 1, []):
+                last_factor(x)
+            for x in tile_slots.get(g - 2, []):
+                if x in GPSIMD_TILES:
+                    gpsimd_sum(x)
+                    gpsimd_difference(x)
+            for x in tile_slots.get(g - 3, []):
+                if x in GPSIMD_TILES:
+                    store(*tiles[x], ys[x][:, 1])
+            for x in tile_slots.get(g, []):
+                if g <= TURNED_SLOTS:
+                    multiply(x, "drn", DRN_BUFS)
+                else:
+                    tag, bufs = (("drn", DRN_BUFS), ("diff", DIFF_BUFS), ("mask", MASK_BUFS))[next_tag % 3]
+                    next_tag += 1
+                    multiply(x, tag, bufs)
+            if 0 <= g < SLOTS:
+                for k in range(2):
+                    if g < TURNED_SLOTS:
+                        mask(g, k)
+                for k, slot in regroup_slot.items():
+                    if slot == g and k not in VECTOR_REGROUPS:
+                        regroup_sn(k)
+                if g == G1_SLOT:
+                    regroup_g(1)
+            if 0 <= g < SLOTS:
+                if g in UNIT3_LOADS:
+                    for h in UNIT3_LOADS[g]:
+                        load_head(3, h)
+                if g in UNIT4_LOADS:
+                    load_head(4, UNIT4_LOADS[g])
+                if 16 <= g < 24:
+                    load_ro(g - 16)
+                while n_s < len(sn_tiles) and regroup_slot[n_s] - 6 <= g:
+                    load_sn_rows(n_s)
+                    n_s += 1

@@ -48,6 +48,7 @@ GPSIMD_REGROUPS = ()
 def SN_SLOTS(q):
     return 2 * q + 1
 
+
 G1_SLOT = 6
 SN_STEP = 2
 DIFF_BUFS = 3
@@ -56,9 +57,13 @@ DRN_BUFS = 2
 TURNED_BUFS = 4
 Z_TILES = ()
 Z_LAG = 0
-GROUPED_BUFS = 5
+GROUPED_BUFS = 4
+ROWS_BUFS = 5
+NEG_BY_S = (3, 4)
+NEGATE_SLOTS = {1: 1, 2: 5, 3: 11, 4: 19}
+S_SCALE = ()
 HEAD_Q_SLOT = 1
-B2_TILES = tuple(range(16, 32))
+B2_TILES = tuple(range(12, 32))
 TILES_LAST = False
 PRODUCT_LATE = 0
 TB_LAG = 1
@@ -79,7 +84,7 @@ def tile_multiheaddistance_v_kernel(tc, batch_s, batch_ro, dist, inv_s, inv_ro, 
     nc = tc.nc
 
     with tc.tile_pool(name="keep", bufs=1) as keep, tc.tile_pool(name="stream", bufs=STREAM_BUFS) as stream, tc.tile_pool(
-        name="rows", bufs=6
+        name="rows", bufs=ROWS_BUFS
     ) as rows_pool, tc.tile_pool(name="work", bufs=1) as work, tc.psum_pool(name="psum", bufs=1) as psum, tc.manual_schedule():
         dd_codes = keep.tile([P, HEADS, SLOT], U32, align_bytes=64)
         dd_scales = keep.tile([P, HEADS, SLOT], U8, align_bytes=64)
@@ -106,6 +111,7 @@ def tile_multiheaddistance_v_kernel(tc, batch_s, batch_ro, dist, inv_s, inv_ro, 
         heads = {}
         best = {}
         minus_top = {}
+        minus_last = {}
         diffs = {}
         turned = {}
         words = {}
@@ -165,6 +171,22 @@ def tile_multiheaddistance_v_kernel(tc, batch_s, batch_ro, dist, inv_s, inv_ro, 
             b = best[u]
             if i < 2:
                 nc.vector.tensor_tensor(out=b[:, i], in0=head(u, 2 * i), in1=head(u, 2 * i + 1), op=ALU.max)
+            elif u in NEG_BY_S:
+                if i < 5:
+                    nc.vector.tensor_tensor(out=b[:, i % 2], in0=b[:, i % 2], in1=head(u, i + 2), op=ALU.max)
+                elif i == 5:
+                    nc.vector.tensor_tensor(out=b[:, 0], in0=b[:, 0], in1=b[:, 1], op=ALU.max)
+                elif i == 6:
+                    tile = work.tile([P, PACK, width], F32, tag="minus_top", bufs=2)
+                    nc.vector.scalar_tensor_tensor(
+                        out=tile[:].rearrange("p j m -> p (j m)"),
+                        in0=b[:, 0].rearrange("p j m -> p (j m)"),
+                        scalar=-1.0,
+                        in1=minus_last[u][:].rearrange("p j m -> p (j m)"),
+                        op0=ALU.mult,
+                        op1=ALU.min,
+                    )
+                    minus_top[u] = tile
             elif i < 6:
                 nc.vector.tensor_tensor(out=b[:, i % 2], in0=b[:, i % 2], in1=head(u, i + 2), op=ALU.max)
             elif i == 6:
@@ -173,6 +195,12 @@ def tile_multiheaddistance_v_kernel(tc, batch_s, batch_ro, dist, inv_s, inv_ro, 
                 tile = work.tile([P, PACK, width], F32, tag="minus_top", bufs=2)
                 nc.vector.tensor_scalar_mul(out=tile[:], in0=b[:, 0], scalar1=-1.0)
                 minus_top[u] = tile
+
+        def negate_last(u):
+            width = UNITS[u][2]
+            tile = work.tile([P, PACK, width], F32, tag="minus_last", bufs=1)
+            nc.scalar.mul(out=tile[:], in_=head(u, HEADS - 1), mul=-1.0)
+            minus_last[u] = tile
 
         def turn_and_subtract(g, k):
             u, pairs = slots[g]
@@ -217,13 +245,13 @@ def tile_multiheaddistance_v_kernel(tc, batch_s, batch_ro, dist, inv_s, inv_ro, 
             else:
                 factor = words[g][:].rearrange("p b m u -> p (b m u)").bitcast(BF16)
             n = min(width * PACK, SLOT)
-            for first in range(0, SLOT, n):
-                nc.vector.tensor_tensor(
-                    out=dd_of(g)[:, first : first + n],
-                    in0=factor[:, first : first + n],
-                    in1=g_grouped[:, c, m0 * PACK : m0 * PACK + n],
-                    op=ALU.mult,
-                )
+            count = SLOT // n
+            nc.vector.tensor_tensor(
+                out=dd_of(g).rearrange("p (k e) -> p k e", k=count),
+                in0=factor.rearrange("p (k e) -> p k e", k=count),
+                in1=g_grouped[:, c, m0 * PACK : m0 * PACK + n].unsqueeze(1).to_broadcast([P, count, n]),
+                op=ALU.mult,
+            )
 
         def compare(g):
             u, pairs = slots[g]
@@ -250,6 +278,10 @@ def tile_multiheaddistance_v_kernel(tc, batch_s, batch_ro, dist, inv_s, inv_ro, 
 
         def scale_sn(k, rows):
             c, h = sn_tiles[k]
+            if k in S_SCALE:
+                for j in rows:
+                    nc.scalar.activation(out=raws[k][:, j], in_=raws[k][:, j], func=COPY, scale=inv_s_sb[:, c, j, h : h + 1])
+                return
             for j in rows:
                 nc.vector.tensor_scalar_mul(out=raws[k][:, j], in0=raws[k][:, j], scalar1=inv_s_sb[:, c, j, h : h + 1])
 
@@ -504,6 +536,9 @@ def tile_multiheaddistance_v_kernel(tc, batch_s, batch_ro, dist, inv_s, inv_ro, 
                     tag, bufs = (("drn", DRN_BUFS), ("diff", DIFF_BUFS), ("mask", MASK_BUFS))[next_tag % 3]
                     next_tag += 1
                     multiply(x, tag, bufs)
+            for u1, slot in NEGATE_SLOTS.items():
+                if slot == g and u1 in NEG_BY_S:
+                    negate_last(u1)
             if 0 <= g < SLOTS:
                 for k in range(2):
                     if g < TURNED_SLOTS:

@@ -24,7 +24,7 @@ M_TILES = M_ROWS // P
 UNITS = ((0, 0, 128), (0, 128, 128), (0, 256, 256), (1, 0, 256), (1, 256, 256))
 SLOT = 2 * P * PACK
 GROUP = 4
-RUN = 4
+RUN = 8
 BIG = 2.0 ** 100
 STREAM_BUFS = 16
 RO_HEADS = 4

@@ -54,16 +54,16 @@ SN_STEP = 2
 DIFF_BUFS = 3
 MASK_BUFS = 3
 DRN_BUFS = 2
-TURNED_BUFS = 4
+TURNED_BUFS = 6
 Z_TILES = ()
 Z_LAG = 0
-GROUPED_BUFS = 4
+GROUPED_BUFS = 5
 ROWS_BUFS = 5
 NEG_BY_S = (3, 4)
 NEGATE_SLOTS = {1: 1, 2: 5, 3: 11, 4: 19}
 S_SCALE = ()
 HEAD_Q_SLOT = 1
-B2_TILES = tuple(range(12, 32))
+B2_TILES = tuple(range(18, 32))
 TILES_LAST = False
 PRODUCT_LATE = 0
 TB_LAG = 1

import concourse.mybir as mybir
from concourse.masks import make_identity

F32 = mybir.dt.float32
BF16 = mybir.dt.bfloat16
U32 = mybir.dt.uint32
U8 = mybir.dt.uint8
E4M3_X4 = mybir.dt.float8_e4m3fn_x4
E5M2_X4 = mybir.dt.float8_e5m2_x4
ALU = mybir.AluOpType
COPY = mybir.ActivationFunctionType.Copy
RELU = mybir.ActivationFunctionType.Relu

P = 128
PACK = 4
K_PASS = P * PACK
N_ROWS = 1024
M_ROWS = 512
HEADS = 8
HEAD_DIM = 512
PASSES = N_ROWS // K_PASS
M_TILES = M_ROWS // P

UNITS = ((0, 0, 128), (0, 128, 128), (0, 256, 256), (1, 0, 256), (1, 256, 256))
SLOT = 2 * P * PACK
GROUP = 4
RUN = 8
BIG = 2.0 ** 100
STREAM_BUFS = 16
RO_HEADS = 4
SN_HEAD = 1
HEAD_LOADS = "a a a a g a a a a s b b b b s b b b b s d d s d d s d d s d d s g"
HEAD_WORK = "m0 m1 g m2 m3 m4 m5 m6 m7 c0 r0"
VECTOR_COMPARES = {}
MAXIMUM_SLOTS = (
    (0, 0, 1, 1, 1, 2, 2, 2),
    (3, 3, 4, 4, 5, 5, 6, 6),
    (7, 8, 9, 10, 11, 12, 13, 13),
    (14, 15, 16, 17, 18, 19, 20, 21),
)
FIRST_TILE = 23
TILE_COUNTS = (1, 1, 1, 1, 1, 1, 1, 1, 1, 1, 1, 3, 3, 3, 3, 3, 3, 3)
GPSIMD_TILES = (0, 4, 8, 12, 15, 18, 21, 24)
UNIT3_LOADS = {4: (0, 1), 5: (2, 3), 6: (4, 5), 7: (6, 7)}
UNIT4_LOADS = {8: 0, 9: 1, 10: 2, 11: 3, 12: 4, 13: 5, 14: 6, 15: 7}
VECTOR_REGROUPS = ()
GPSIMD_REGROUPS = ()
def SN_SLOTS(q):
    return 2 * q + 1


G1_SLOT = 6
SN_STEP = 2
DIFF_BUFS = 3
MASK_BUFS = 3
DRN_BUFS = 2
TURNED_BUFS = 6
Z_TILES = ()
Z_LAG = 0
GROUPED_BUFS = 5
ROWS_BUFS = 5
NEG_BY_S = (3, 4)
NEGATE_SLOTS = {1: 1, 2: 5, 3: 11, 4: 19}
S_SCALE = ()
HEAD_Q_SLOT = 1
B2_TILES = tuple(range(18, 32))
TILES_LAST = False
PRODUCT_LATE = 0
TB_LAG = 1
LAG = 2

FLOPS = 2 * HEADS * M_ROWS * N_ROWS * HEAD_DIM


def by_rows_view(ap):
    return ap.rearrange("p j (r i) -> p r j i", i=RUN)


def grouped_view(ap):
    return ap.rearrange("p (r i j) -> p r j i", i=RUN, j=PACK)


def tile_multiheaddistance_v_kernel(tc, batch_s, batch_ro, dist, inv_s, inv_ro, grad_out, out):
    nc = tc.nc

    with tc.tile_pool(name="keep", bufs=1) as keep, tc.tile_pool(name="stream", bufs=STREAM_BUFS) as stream, tc.tile_pool(
        name="rows", bufs=ROWS_BUFS
    ) as rows_pool, tc.tile_pool(name="work", bufs=1) as work, tc.psum_pool(name="psum", bufs=1) as psum, tc.manual_schedule():
        dd_codes = keep.tile([P, HEADS, SLOT], U32, align_bytes=64)
        dd_scales = keep.tile([P, HEADS, SLOT], U8, align_bytes=64)
        sn_codes = keep.tile([P, PASSES, HEADS, HEAD_DIM], U32, align_bytes=64)
        sn_scales = keep.tile([P, PASSES, HEADS, HEAD_DIM], U8, align_bytes=64)
        inv_s_sb = keep.tile([P, PASSES, PACK, HEADS], F32)
        inv_ro_sb = keep.tile([P, M_TILES, HEADS], F32)
        neg_inv_ro_sq = keep.tile([P, M_TILES, HEADS], F32)
        coef_v = keep.tile([P, M_TILES, HEADS], F32)
        coef_g = keep.tile([P, M_TILES, HEADS], F32)
        g_grouped = keep.tile([P, PASSES, PACK * M_ROWS], BF16)
        identity = keep.tile([P, P], F32)
        make_identity(nc, identity[:])

        slots = []
        for u, (c, m0, width) in enumerate(UNITS):
            pairs = [(h, b) for h in range(HEADS) for b in range(width // P)]
            slots += [(u, pairs[k : k + 2]) for k in range(0, len(pairs), 2)]
        sn_tiles = [(c, h) for h in range(HEADS) for c in range(PASSES)]
        SLOTS = len(slots)
        TURNED_SLOTS = SLOTS - len(VECTOR_COMPARES)
        tiles = [(t, h) for part in range(2) for h in range(HEADS) for t in (2 * part, 2 * part + 1)]

        heads = {}
        best = {}
        minus_top = {}
        minus_last = {}
        diffs = {}
        turned = {}
        words = {}
        dd_tiles = {}
        raws = {}
        g_raws = {}
        groupeds = {}
        ro_tiles = []
        drns = {}
        results = {}
        ys = {}

        def load_head(u, h):
            c, m0, width = UNITS[u]
            if u == 1:
                tile = heads[(0, h)][0]
            else:
                tile = stream.tile([P, PACK * 256], F32, tag="stream")
            first = PACK * P if u == 1 else 0
            view = tile[:, first : first + PACK * width].rearrange("p (j m) -> p j m", j=PACK)
            rows = dist[h, c * K_PASS : (c + 1) * K_PASS, m0 : m0 + width]
            nc.sync.dma_start(out=view, in_=rows.rearrange("(p j) m -> p j m", j=PACK))
            heads[(u, h)] = (tile, view)

        def head(u, h):
            return heads[(u, h)][1]

        def load_rows(src, c, columns):
            raw = rows_pool.tile([P, PACK, HEAD_DIM], BF16, tag="raw")
            nc.sync.dma_start(
                out=raw[:], in_=src[c * K_PASS : (c + 1) * K_PASS, columns].rearrange("(p j) w -> p j w", j=PACK)
            )
            return raw

        def load_sn_rows(k):
            c, h = sn_tiles[k]
            raws[k] = load_rows(batch_s, c, slice(h * HEAD_DIM, (h + 1) * HEAD_DIM))

        def load_g(c):
            g_raws[c] = load_rows(grad_out, c, slice(0, M_ROWS))

        def load_ro(k):
            t, half = k // (HEADS // RO_HEADS), k % (HEADS // RO_HEADS)
            tile = stream.tile([P, RO_HEADS * HEAD_DIM], BF16, tag="stream")
            width = RO_HEADS * HEAD_DIM
            nc.sync.dma_start(out=tile[:], in_=batch_ro[t * P : (t + 1) * P, half * width : (half + 1) * width])
            ro_tiles.append(tile)

        def regroup_g(c):
            nc.scalar.copy(out=grouped_view(g_grouped[:, c]), in_=by_rows_view(g_raws[c][:]))

        def maximum_step(u, i):
            width = UNITS[u][2]
            if i == 0:
                tile = work.tile([P, 2, PACK, width], F32, tag="best")
                best[u] = tile
            b = best[u]
            if i < 2:
                nc.vector.tensor_tensor(out=b[:, i], in0=head(u, 2 * i), in1=head(u, 2 * i + 1), op=ALU.max)
            elif u in NEG_BY_S:
                if i < 5:
                    nc.vector.tensor_tensor(out=b[:, i % 2], in0=b[:, i % 2], in1=head(u, i + 2), op=ALU.max)
                elif i == 5:
                    nc.vector.tensor_tensor(out=b[:, 0], in0=b[:, 0], in1=b[:, 1], op=ALU.max)
                elif i == 6:
                    tile = work.tile([P, PACK, width], F32, tag="minus_top", bufs=2)
                    nc.vector.scalar_tensor_tensor(
                        out=tile[:].rearrange("p j m -> p (j m)"),
                        in0=b[:, 0].rearrange("p j m -> p (j m)"),
                        scalar=-1.0,
                        in1=minus_last[u][:].rearrange("p j m -> p (j m)"),
                        op0=ALU.mult,
                        op1=ALU.min,
                    )
                    minus_top[u] = tile
            elif i < 6:
                nc.vector.tensor_tensor(out=b[:, i % 2], in0=b[:, i % 2], in1=head(u, i + 2), op=ALU.max)
            elif i == 6:
                nc.vector.tensor_tensor(out=b[:, 0], in0=b[:, 0], in1=b[:, 1], op=ALU.max)
            else:
                tile = work.tile([P, PACK, width], F32, tag="minus_top", bufs=2)
                nc.vector.tensor_scalar_mul(out=tile[:], in0=b[:, 0], scalar1=-1.0)
                minus_top[u] = tile

        def negate_last(u):
            width = UNITS[u][2]
            tile = work.tile([P, PACK, width], F32, tag="minus_last", bufs=1)
            nc.scalar.mul(out=tile[:], in_=head(u, HEADS - 1), mul=-1.0)
            minus_last[u] = tile

        def turn_and_subtract(g, k):
            u, pairs = slots[g]
            h, b = pairs[k]
            cols = slice(b * P, (b + 1) * P)
            diff = psum.tile([P, PACK, P], F32, tag="diff", bufs=DIFF_BUFS)
            for j in range(PACK):
                nc.tensor.matmul(
                    out=diff[:, j], lhsT=head(u, h)[:, j, cols], rhs=identity[:], is_transpose=True, start=True, stop=False
                )
                nc.tensor.matmul(
                    out=diff[:, j], lhsT=minus_top[u][:, j, cols], rhs=identity[:], is_transpose=True, start=False, stop=True
                )
            diffs[(g, k)] = diff

        def mask(g, k):
            tile = work.tile([P, 2, P, 2], BF16, tag="turned", bufs=TURNED_BUFS)
            nc.scalar.activation(
                out=tile[:], in_=diffs[(g, k)][:].rearrange("m (u e) p -> m u p e", e=2), func=RELU, scale=BIG, bias=1.0
            )
            turned[(g, k)] = tile

        def turn_back(g, k):
            if k == 0:
                tile = psum.tile([P, 2, P, 2], F32, tag="mask", bufs=MASK_BUFS)
                words[g] = tile
            rows = turned[(g, k)][:].rearrange("m u p e -> m (u p e)").bitcast(F32)
            for u2 in range(2):
                nc.tensor.transpose(out=words[g][:, k, :, u2], in_=rows[:, u2 * P : (u2 + 1) * P], identity=identity[:])

        def dd_of(g):
            if g // GROUP not in dd_tiles:
                tile = work.tile([P, GROUP, SLOT], BF16, align_bytes=64, tag="dd", bufs=2)
                dd_tiles[g // GROUP] = tile
            return dd_tiles[g // GROUP][:, g % GROUP]

        def product(g):
            u, pairs = slots[g]
            c, m0, width = UNITS[u]
            if g in VECTOR_COMPARES:
                factor = dd_of(g)
            else:
                factor = words[g][:].rearrange("p b m u -> p (b m u)").bitcast(BF16)
            n = min(width * PACK, SLOT)
            count = SLOT // n
            nc.vector.tensor_tensor(
                out=dd_of(g).rearrange("p (k e) -> p k e", k=count),
                in0=factor.rearrange("p (k e) -> p k e", k=count),
                in1=g_grouped[:, c, m0 * PACK : m0 * PACK + n].unsqueeze(1).to_broadcast([P, count, n]),
                op=ALU.mult,
            )

        def compare(g):
            u, pairs = slots[g]
            nc.vector.tensor_tensor(
                out=grouped_view(dd_of(g)),
                in0=by_rows_view(head(u, pairs[0][0])),
                in1=by_rows_view(best[u][:, 0]),
                op=ALU.is_equal,
            )

        def quantise_dd(k):
            nc.vector.quantize_mx(
                out=dd_codes[:, k].bitcast(E5M2_X4),
                scales=dd_scales[:, k],
                in_=dd_tiles[k][:].rearrange("p h e -> p (h e)"),
            )

        def dd_columns(c, t, h):
            for g, (u, pairs) in enumerate(slots):
                for k, (h2, b) in enumerate(pairs):
                    if UNITS[u][0] == c and UNITS[u][1] + b * P == t * P and h2 == h:
                        first = (g % GROUP) * 2 * P + k * P
                        return g // GROUP, slice(first, first + P)

        def scale_sn(k, rows):
            c, h = sn_tiles[k]
            if k in S_SCALE:
                for j in rows:
                    nc.scalar.activation(out=raws[k][:, j], in_=raws[k][:, j], func=COPY, scale=inv_s_sb[:, c, j, h : h + 1])
                return
            for j in rows:
                nc.vector.tensor_scalar_mul(out=raws[k][:, j], in0=raws[k][:, j], scalar1=inv_s_sb[:, c, j, h : h + 1])

        def regroup_sn(k, engine=None):
            tile = work.tile([P, PACK * HEAD_DIM], BF16, align_bytes=64, tag="sn_grouped", bufs=GROUPED_BUFS)
            groupeds[k] = tile
            if k in GPSIMD_REGROUPS:
                nc.gpsimd.tensor_scalar(
                    out=tile[:].rearrange("p (d j) -> p d j", j=PACK),
                    in0=raws[k][:].rearrange("p j d -> p d j"),
                    scalar1=1.0,
                    scalar2=0.0,
                    op0=ALU.mult,
                    op1=ALU.add,
                )
            elif k in VECTOR_REGROUPS:
                nc.vector.tensor_copy(out=grouped_view(tile[:]), in_=by_rows_view(raws[k][:]))
            else:
                nc.scalar.copy(out=grouped_view(tile[:]), in_=by_rows_view(raws[k][:]))

        def quantise_sn(k):
            c, h = sn_tiles[k]
            nc.vector.quantize_mx(out=sn_codes[:, c, h].bitcast(E4M3_X4), scales=sn_scales[:, c, h], in_=groupeds[k][:])

        def ro_of(t, h):
            k = h % RO_HEADS
            return ro_tiles[t * (HEADS // RO_HEADS) + h // RO_HEADS][:, k * HEAD_DIM : (k + 1) * HEAD_DIM]

        def store(t, h, result):
            nc.sync.dma_start(out=out[t * P : (t + 1) * P, h * HEAD_DIM : (h + 1) * HEAD_DIM], in_=result)

        def multiply(x, tag, bufs):
            t, h = tiles[x]
            drn = psum.tile([P, HEAD_DIM], F32, tag=tag, bufs=bufs)
            for c in range(PASSES):
                group, columns = dd_columns(c, t, h)
                nc.tensor.matmul_mx(
                    out=drn[:],
                    lhsT=dd_codes[:, group, columns].bitcast(E5M2_X4),
                    lhsT_scale=dd_scales[:, group, columns],
                    rhs=sn_codes[:, c, h].bitcast(E4M3_X4),
                    rhs_scale=sn_scales[:, c, h],
                    start=(c == 0),
                    stop=(c == PASSES - 1),
                )
            drns[x] = drn

        def vector_sum(x):
            t, h = tiles[x]
            unused = work.tile([P, HEAD_DIM], BF16, tag="unused", bufs=1)
            nc.vector.scalar_tensor_tensor(
                out=unused[:],
                in0=drns[x][:],
                scalar=neg_inv_ro_sq[:, t, h : h + 1],
                in1=ro_of(t, h),
                op0=ALU.mult,
                op1=ALU.mult,
                accum_out=coef_v[:, t, h : h + 1],
            )

        def vector_difference(x):
            t, h = tiles[x]
            if x in late_results:
                result = stream.tile([P, HEAD_DIM], F32, tag="stream")
            else:
                result = rows_pool.tile([P, HEAD_DIM], F32, tag="raw")
            nc.vector.scalar_tensor_tensor(
                out=result[:], in0=ro_of(t, h), scalar=coef_v[:, t, h : h + 1], in1=drns[x][:], op0=ALU.mult, op1=ALU.add
            )
            results[x] = result

        def last_factor(x):
            t, h = tiles[x]
            nc.scalar.activation(out=results[x][:], in_=results[x][:], func=COPY, scale=inv_ro_sb[:, t, h : h + 1])
            store(t, h, results[x][:])

        def gpsimd_y(x):
            t, h = tiles[x]
            y = work.tile([P, 2, HEAD_DIM], F32, align_bytes=64, tag="sn_grouped", bufs=GROUPED_BUFS)
            nc.scalar.activation(out=y[:, 0], in_=drns[x][:], func=COPY, scale=inv_ro_sb[:, t, h : h + 1])
            ys[x] = y

        def gpsimd_products(x):
            nc.gpsimd.tensor_tensor(out=ys[x][:, 1], in0=ys[x][:, 0], in1=ro_of(*tiles[x]), op=ALU.mult)

        def gpsimd_sum(x):
            t, h = tiles[x]
            nc.scalar.activation(
                out=ys[x][:, 1],
                in_=ys[x][:, 1],
                func=COPY,
                scale=neg_inv_ro_sq[:, t, h : h + 1],
                accum_out=coef_g[:, t, h : h + 1],
            )

        def gpsimd_difference(x):
            t, h = tiles[x]
            if x in B2_TILES:
                nc.scalar.activation(out=ys[x][:, 1], in_=ro_of(t, h), func=COPY, scale=coef_g[:, t, h : h + 1])
            else:
                nc.gpsimd.tensor_scalar(
                    out=ys[x][:, 1], in0=ro_of(t, h), scalar1=coef_g[:, t, h : h + 1], scalar2=0.0, op0=ALU.mult, op1=ALU.add
                )
            nc.gpsimd.tensor_tensor(out=ys[x][:, 1], in0=ys[x][:, 1], in1=ys[x][:, 0], op=ALU.add)

        def gpsimd_z(x):
            t, h = tiles[x]
            z = work.tile([P, HEAD_DIM], F32, align_bytes=64, tag="z", bufs=2)
            nc.gpsimd.tensor_scalar(out=z[:], in0=ro_of(t, h), scalar1=coef_v[:, t, h : h + 1], scalar2=0.0, op0=ALU.mult, op1=ALU.add)
            ys[x] = z

        def z_difference(x):
            t, h = tiles[x]
            if x in late_results:
                result = stream.tile([P, HEAD_DIM], F32, tag="stream")
            else:
                result = rows_pool.tile([P, HEAD_DIM], F32, tag="raw")
            nc.vector.scalar_tensor_tensor(
                out=result[:], in0=drns[x][:], scalar=inv_ro_sb[:, t, h : h + 1], in1=ys[x][:], op0=ALU.mult, op1=ALU.add
            )
            store(t, h, result[:])

        nc.sync.dma_start(
            out=inv_s_sb[:].rearrange("p c j h -> p c (j h)"),
            in_=inv_s.rearrange("(c p j) h -> p c (j h)", c=PASSES, j=PACK),
        )
        n_s, n_g = 0, 0
        n_u = {"a": 0, "b": 0, "d": 0}
        for what in HEAD_LOADS.split():
            if what == "s":
                load_sn_rows(n_s)
                n_s += 1
            elif what in n_u:
                load_head("abd".index(what), n_u[what])
                n_u[what] += 1
            elif what == "g":
                load_g(n_g)
                n_g += 1
        nc.sync.dma_start(out=inv_ro_sb[:], in_=inv_ro.rearrange("(t p) h -> p t h", p=P))

        all_rows = range(PACK)
        for what in HEAD_WORK.split():
            if what[0] == "c":
                scale_sn(int(what[1:]), all_rows)
            elif what[0] == "r":
                regroup_sn(int(what[1:]))
            elif what[0] == "q":
                quantise_sn(int(what[1:]))
            elif what[0] == "m":
                maximum_step(0, int(what[1:]))
            else:
                regroup_g(0)
        head_q = [int(w[1:]) for w in HEAD_WORK.split() if w[0] == "q"]
        head_r = [int(w[1:]) for w in HEAD_WORK.split() if w[0] == "r"]

        tile_slots = {}
        x = 0
        for k, count in enumerate(TILE_COUNTS):
            tile_slots[FIRST_TILE + k] = [y for y in range(x, x + count) if y < len(tiles)]
            x += count
        last_slot = FIRST_TILE + len(TILE_COUNTS) + 3

        regroup_slot = {SN_HEAD + q: SN_SLOTS(q) for q in range(len(sn_tiles) - SN_HEAD)}
        next_tag = 0

        pending = []
        diff_slot = {}
        late_results = [x for x in range(len(tiles)) if x not in GPSIMD_TILES][-8:]

        def vector_tiles(g):
            for x in tile_slots.get(g - 1, []):
                if x not in GPSIMD_TILES:
                    vector_sum(x)
                    if x in Z_TILES:
                        gpsimd_z(x)
                    if pending:
                        finish(pending.pop(), g)
                    pending.append(x)
            if pending and not any(x not in GPSIMD_TILES for x in tile_slots.get(g - 1, [])) and (g > FIRST_TILE + 1):
                finish(pending.pop(), g)

        def finish(y, g):
            if y in Z_TILES:
                z_difference(y)
            else:
                vector_difference(y)
                diff_slot.setdefault(g, []).append(y)

        for g in range(last_slot + 1):
            if not (PRODUCT_LATE and g >= PRODUCT_LATE) and 0 <= g - LAG < TURNED_SLOTS:
                product(g - LAG)
            if not TILES_LAST:
                vector_tiles(g)
            for u1 in range(1, len(UNITS)):
                for i1 in range(HEADS):
                    if MAXIMUM_SLOTS[u1 - 1][i1] == g:
                        maximum_step(u1, i1)
            for k, slot in regroup_slot.items():
                if slot - 1 == g and slot - 2 < 0:
                    scale_sn(k, all_rows)
                elif slot - 2 == g:
                    scale_sn(k, (0, 1))
                elif slot - 1 == g:
                    scale_sn(k, (2, 3))
            for slot1, slot in VECTOR_COMPARES.items():
                if slot + 1 == g:
                    product(slot1)
                if slot == g:
                    compare(slot1)
            done = g - LAG - 1
            if 0 <= done < TURNED_SLOTS and (done % GROUP == GROUP - 1 or done == TURNED_SLOTS - 1):
                quantise_dd(done // GROUP)
            if g == HEAD_Q_SLOT:
                for k in head_r:
                    if k not in head_q:
                        quantise_sn(k)
            for k, slot in regroup_slot.items():
                if slot == g and k in VECTOR_REGROUPS:
                    regroup_sn(k)
                if slot + 2 == g:
                    quantise_sn(k)
            if g == FIRST_TILE - 2:
                nc.vector.scalar_tensor_tensor(
                    out=neg_inv_ro_sq[:], in0=inv_ro_sb[:], scalar=-1.0, in1=inv_ro_sb[:], op0=ALU.mult, op1=ALU.mult
                )
            if PRODUCT_LATE and g >= PRODUCT_LATE and 0 <= g - LAG < TURNED_SLOTS:
                product(g - LAG)
            if TILES_LAST:
                vector_tiles(g)
            for k in range(2):
                if 0 <= g < TURNED_SLOTS:
                    turn_and_subtract(g, k)
                if 0 <= g - TB_LAG < TURNED_SLOTS:
                    turn_back(g - TB_LAG, k)
            for x in tile_slots.get(g - 1, []):
                if x in GPSIMD_TILES:
                    gpsimd_y(x)
                    gpsimd_products(x)
            for x in diff_slot.get(g - 1, []):
                last_factor(x)
            for x in tile_slots.get(g - 2, []):
                if x in GPSIMD_TILES:
                    gpsimd_sum(x)
                    gpsimd_difference(x)
            for x in tile_slots.get(g - 3, []):
                if x in GPSIMD_TILES:
                    store(*tiles[x], ys[x][:, 1])
            for x in tile_slots.get(g, []):
                if g <= TURNED_SLOTS:
                    multiply(x, "drn", DRN_BUFS)
                else:
                    tag, bufs = (("drn", DRN_BUFS), ("diff", DIFF_BUFS), ("mask", MASK_BUFS))[next_tag % 3]
                    next_tag += 1
                    multiply(x, tag, bufs)
            for u1, slot in NEGATE_SLOTS.items():
                if slot == g and u1 in NEG_BY_S:
                    negate_last(u1)
            if 0 <= g < SLOTS:
                for k in range(2):
                    if g < TURNED_SLOTS:
                        mask(g, k)
                for k, slot in regroup_slot.items():
                    if slot == g and k not in VECTOR_REGROUPS:
                        regroup_sn(k)
                if g == G1_SLOT:
                    regroup_g(1)
            if 0 <= g < SLOTS:
                if g in UNIT3_LOADS:
                    for h in UNIT3_LOADS[g]:
                        load_head(3, h)
                if g in UNIT4_LOADS:
                    load_head(4, UNIT4_LOADS[g])
                if 16 <= g < 24:
                    load_ro(g - 16)
                while n_s < len(sn_tiles) and regroup_slot[n_s] - 6 <= g:
                    load_sn_rows(n_s)
                    n_s += 1
